import numpy as np
import ml_dtypes


def mxq(x, axis, fmt="e4m3"):
    dtype, down = {"e4m3": (ml_dtypes.float8_e4m3fn, 7), "e5m2": (ml_dtypes.float8_e5m2, 14)}[fmt]
    v = np.moveaxis(np.asarray(x, np.float32).astype(ml_dtypes.bfloat16).astype(np.float64), axis, -1)
    blocks = v.reshape(v.shape[:-1] + (-1, 32))
    amax = np.abs(blocks).max(-1, keepdims=True)
    byte = np.maximum(np.where(amax > 0, np.frexp(amax)[1] - 1 + 127, 0) - down, 1)
    scale = np.exp2(byte - 127.0)
    codes = (blocks / scale).astype(np.float32).astype(dtype).astype(np.float64)
    return np.moveaxis((codes * scale).reshape(v.shape), -1, axis)


WIDE = False


def mx_kscale(k):
    if not WIDE:
        return np.ones(k)
    levels = np.array([20, -20, 10, -10, 0])
    a = np.random.permutation(np.resize(levels, k // 512 * 4)).reshape(k // 512, 4)
    idx = np.arange(k)
    return np.exp2(a[idx // 512, idx % 128 // 32])


BF16 = ml_dtypes.bfloat16


def bf(x):
    return np.asarray(x, np.float32).astype(BF16)


def f64(x):
    return np.asarray(x).astype(np.float64)


GRID_SIZE = 10
K = 3
G = GRID_SIZE + K
IN_FEAT = 512
OUT_FEAT = 512
BATCH = 1024


def make_grid(grid_size=GRID_SIZE, k=K):
    h = 4.0 / grid_size
    grid = np.linspace(-2.0, 2.0, grid_size + 1)
    pad = np.linspace(-2.0 - k * h, -2.0 - h, k)
    pad_end = np.linspace(2.0 + h, 2.0 + k * h, k)
    return np.concatenate([pad, grid, pad_end])


def b_splines(x, grid, k=K):
    x = x[..., None]
    bases = ((x >= grid[:-1]) & (x < grid[1:])).astype(np.float64)
    for p in range(1, k + 1):
        t1 = (x - grid[:-p - 1]) / (grid[p:-1] - grid[:-p - 1] + 1e-8) * bases[..., :-1]
        t2 = (grid[p + 1:] - x) / (grid[p + 1:] - grid[1:-p] + 1e-8) * bases[..., 1:]
        bases = t1 + t2
    return bases


def b_splines_deriv(x, grid, k=K):
    x = x[..., None]
    b = ((x >= grid[:-1]) & (x < grid[1:])).astype(np.float64)
    d = np.zeros_like(b)
    for p in range(1, k + 1):
        den1 = grid[p:-1] - grid[:-p - 1] + 1e-8
        den2 = grid[p + 1:] - grid[1:-p] + 1e-8
        a1 = (x - grid[:-p - 1]) / den1
        a2 = (grid[p + 1:] - x) / den2
        d = b[..., :-1] / den1 + a1 * d[..., :-1] - b[..., 1:] / den2 + a2 * d[..., 1:]
        b = a1 * b[..., :-1] + a2 * b[..., 1:]
    return d


def silu(v):
    return v / (1.0 + np.exp(-v))


def silu_deriv(v):
    sg = 1.0 / (1.0 + np.exp(-v))
    return sg * (1.0 + v * (1.0 - sg))


def setup_inputs():
    u = mx_kscale(OUT_FEAT)
    x = np.random.standard_normal((BATCH, IN_FEAT))
    base_w = np.random.standard_normal((OUT_FEAT, IN_FEAT)) * (2.0 / np.sqrt(IN_FEAT)) / u[:, None]
    base_b = np.random.standard_normal(OUT_FEAT) * 0.3
    spline_w = np.random.standard_normal((OUT_FEAT, IN_FEAT, G)) * 0.05 / u[:, None, None]
    g = np.random.standard_normal((BATCH, OUT_FEAT)) * np.exp2(np.random.randint(-12, 1, (BATCH, 1))) * 4.0 * u
    return {"x": bf(x), "base_w": bf(base_w), "base_b": bf(base_b), "spline_w": bf(spline_w), "grad_out": bf(g)}


def reference(x, base_w, base_b, spline_w, grad_out):
    x = f64(x)
    grid = make_grid()
    gq = mxq(f64(grad_out), 1, "e5m2")
    p_base = gq @ mxq(f64(base_w), 0, "e4m3")
    wq = mxq(f64(spline_w), 0, "e4m3")
    p_spl = (gq @ wq.reshape(wq.shape[0], -1)).reshape(x.shape[0], x.shape[1], -1)
    return silu_deriv(x) * p_base + (b_splines_deriv(x, grid) * p_spl).sum(-1)

@@ -1,0 +1,271 @@
+from contextlib import ExitStack
+
+import concourse.bass as bass
+import concourse.masks as masks
+import concourse.mybir as mybir
+import concourse.tile as tile
+
+F32 = mybir.dt.float32
+BF16 = mybir.dt.bfloat16
+I32 = mybir.dt.int32
+U32 = mybir.dt.uint32
+U8 = mybir.dt.uint8
+E4 = mybir.dt.float8_e4m3fn_x4
+E5 = mybir.dt.float8_e5m2_x4
+ALU = mybir.AluOpType
+ACT = mybir.ActivationFunctionType
+
+P = 128
+BATCH = 1024
+IN_F = 512
+OUT_F = 512
+NG = 13
+NT = BATCH // P
+NIB = IN_F // P
+H = 0.4
+CN = 6.0 * H * H / ((H + 1e-8) * (2.0 * H + 1e-8) * (3.0 * H + 1e-8))
+FLOPS = 2 * BATCH * OUT_F * IN_F * (NG + 1)
+BANK_G12 = 12
+BANK_BASE = 13
+
+
+def tile_kanlayer_kernel(tc, x, base_w, base_b, spline_w, grad_out, out):
+    nc = tc.nc
+    with ExitStack() as ctx:
+        keep = ctx.enter_context(tc.tile_pool(name="keep", bufs=1))
+        prel = ctx.enter_context(tc.tile_pool(name="prel", bufs=2))
+        pq = ctx.enter_context(tc.psum_pool(name="pq", bufs=3))
+        psel = ctx.enter_context(tc.psum_pool(name="psel", bufs=2))
+        po = ctx.enter_context(tc.psum_pool(name="po", bufs=1))
+        ptp = ctx.enter_context(tc.psum_pool(name="ptp", bufs=2))
+
+        ident_f = keep.tile([P, P], F32, name="ident_f")
+        masks.make_identity(nc, ident_f[:])
+        ident_b = keep.tile([P, P], BF16, name="ident_b")
+        masks.make_identity(nc, ident_b[:])
+
+        x_sb = keep.tile([P, NT, IN_F], BF16, name="x_sb")
+        x_t = keep.tile([P, NIB, BATCH], BF16, name="x_t")
+        xc_t = keep.tile([P, NIB, BATCH], BF16, name="xc_t")
+        go_codes = keep.tile([P, BATCH], U32, name="go_codes", align_bytes=64)
+        go_scales = keep.tile([P, BATCH], U8, name="go_scales", align_bytes=64)
+        w_codes = keep.tile([P, 14, 512], U32, name="w_codes", align_bytes=64)
+        w_scales = keep.tile([P, 14, 512], U8, name="w_scales", align_bytes=64)
+        base_t = keep.tile([P, NIB, BATCH], F32, name="base_t")
+
+        def weights_chunk(c):
+            src = xc_t[:, :, c * 256 : (c + 1) * 256]
+            fa = prel.tile([P, NIB, 256], F32, tag="fa", name="fa%d" % c)
+            nc.scalar.activation(out=fa[:], in_=src, func=ACT.Abs, scale=2.5)
+            nc.scalar.activation(out=fa[:], in_=fa[:], func=ACT.Abs, bias=-4.0)
+            nc.scalar.activation(out=fa[:], in_=fa[:], func=ACT.Abs, bias=-2.0)
+            h0 = prel.tile([P, NIB, 256], F32, tag="h0", name="h0%d" % c)
+            nc.scalar.activation(out=h0[:], in_=fa[:], func=ACT.Abs, scale=0.5, bias=-0.5)
+            fe = prel.tile([P, NIB, 256], F32, tag="fe", name="fe%d" % c)
+            nc.scalar.activation(out=fe[:], in_=src, func=ACT.Abs, scale=2.5, bias=-1.0)
+            nc.scalar.activation(out=fe[:], in_=fe[:], func=ACT.Abs, bias=-4.0)
+            nc.scalar.activation(out=fe[:], in_=fe[:], func=ACT.Abs, bias=-2.0)
+            nc.scalar.activation(out=fe[:], in_=fe[:], func=ACT.Abs, bias=-2.0)
+            a1 = prel.tile([P, NIB, 256], F32, tag="a1", name="a1%d" % c)
+            nc.scalar.activation(out=a1[:], in_=fe[:], func=ACT.Identity, scale=-1.0, bias=2.0)
+            kk = prel.tile([P, 4, NIB, 256], F32, tag="kk", name="kk%d" % c)
+            nc.vector.scalar_tensor_tensor(out=kk[:, 0], in0=h0[:], scalar=1.5, in1=fa[:], op0=ALU.add, op1=ALU.subtract)
+            nc.vector.scalar_tensor_tensor(out=kk[:, 2], in0=h0[:], scalar=-0.5, in1=fa[:], op0=ALU.add, op1=ALU.add)
+            nc.vector.tensor_tensor(out=kk[:, 1], in0=h0[:], in1=fe[:], op=ALU.subtract)
+            nc.vector.tensor_tensor(out=kk[:, 3], in0=a1[:], in1=h0[:], op=ALU.subtract)
+            nc.vector.scalar_tensor_tensor(out=kk[:, 0], in0=a1[:], scalar=1.0, in1=kk[:, 0], op0=ALU.subtract, op1=ALU.mult)
+            nc.vector.scalar_tensor_tensor(out=kk[:, 2], in0=fe[:], scalar=1.0, in1=kk[:, 2], op0=ALU.subtract, op1=ALU.mult)
+            nc.vector.scalar_tensor_tensor(out=kk[:, 1], in0=fa[:], scalar=1.0, in1=kk[:, 1], op0=ALU.subtract, op1=ALU.mult)
+            nc.vector.scalar_tensor_tensor(out=kk[:, 3], in0=fa[:], scalar=1.0, in1=kk[:, 3], op0=ALU.subtract, op1=ALU.mult)
+            return kk
+
+        dsel = {}
+
+        with tc.tile_pool(name="head", bufs=1) as head:
+            go_sb = head.tile([P, NT, OUT_F], BF16, name="go_sb")
+            nc.sync.dma_start(out=go_sb[:], in_=grad_out.rearrange("(t p) o -> p t o", p=P))
+            nc.sync.dma_start(out=x_sb[:], in_=x.rearrange("(t p) i -> p t i", p=P))
+            braw = head.tile([P, 4, IN_F], BF16, name="braw")
+            for u in range(2):
+                nc.sync.dma_start(
+                    out=braw[:, 2 * u : 2 * u + 2, :],
+                    in_=base_w[256 * u : 256 * u + 256, :].rearrange("(q e) i -> q e i", e=2),
+                )
+            raws = []
+            for ib in range(NIB):
+                raw = head.tile([P, 4, P * NG], BF16, tag="raw", bufs=2, name="raw%d" % ib)
+                for u in range(2):
+                    nc.sync.dma_start(
+                        out=raw[:, 2 * u : 2 * u + 2, :],
+                        in_=spline_w[256 * u : 256 * u + 256, ib * P : (ib + 1) * P, :].rearrange(
+                            "(q e) i g -> q e (i g)", e=2
+                        ),
+                    )
+                raws.append(raw)
+
+            ggo = head.tile([P, BATCH * 4], BF16, name="ggo", align_bytes=64)
+            ggo_f = ggo[:].bitcast(F32).rearrange("p (b u) -> p b u", u=2)
+            for pr in range(NT // 2):
+                gw = ptp.tile([P, 2, 2, P], F32, tag="tp", name="gw%d" % pr)
+                for tl in range(2):
+                    words = go_sb[:, 2 * pr + tl, :].bitcast(F32)
+                    for u in range(2):
+                        nc.tensor.transpose(out=gw[:, tl, u, :], in_=words[:, u * P : (u + 1) * P], identity=ident_f[:])
+                nc.vector.tensor_copy(
+                    out=ggo_f[:, pr * 256 : (pr + 1) * 256, :].rearrange("p (tl b) u -> p tl b u", tl=2),
+                    in_=gw[:].rearrange("p tl u b -> p tl b u"),
+                )
+            for pr in range(NT // 2):
+                nc.vector.quantize_mx(
+                    out=go_codes[:, pr * 256 : (pr + 1) * 256].bitcast(E5),
+                    scales=go_scales[:, pr * 256 : (pr + 1) * 256],
+                    in_=ggo[:, pr * 1024 : (pr + 1) * 1024],
+                )
+
+            xc_sb = head.tile([P, NT, IN_F], BF16, name="xc_sb")
+            nc.gpsimd.tensor_scalar(out=xc_sb[:], in0=x_sb[:], scalar1=3.25, scalar2=-3.25, op0=ALU.min, op1=ALU.max)
+            for ib in range(NIB):
+                tpx = ptp.tile([P, BATCH], BF16, tag="tp", name="tpx%d" % ib)
+                for t in range(NT):
+                    nc.tensor.transpose(out=tpx[:, t * P : (t + 1) * P], in_=x_sb[:, t, ib * P : (ib + 1) * P], identity=ident_b[:])
+                nc.scalar.copy(out=x_t[:, ib, :], in_=tpx[:])
+            for ib in range(NIB):
+                tpc = ptp.tile([P, BATCH], BF16, tag="tp", name="tpc%d" % ib)
+                for t in range(NT):
+                    nc.tensor.transpose(out=tpc[:, t * P : (t + 1) * P], in_=xc_sb[:, t, ib * P : (ib + 1) * P], identity=ident_b[:])
+                nc.scalar.copy(out=xc_t[:, ib, :], in_=tpc[:])
+
+            bgrp = head.tile([P, 2048], BF16, tag="grp", bufs=3, name="bgrp", align_bytes=64)
+            nc.vector.tensor_copy(
+                out=bgrp[:].rearrange("p (c i t) -> p c t i", i=4, t=4),
+                in_=braw[:].rearrange("p t (c i) -> p c t i", i=4),
+            )
+            nc.vector.quantize_mx(out=w_codes[:, BANK_BASE, :].bitcast(E4), scales=w_scales[:, BANK_BASE, :], in_=bgrp[:])
+
+            for ib in range(NIB):
+                sg = head.tile([P, BATCH], F32, tag="sg", bufs=2, name="sg%d" % ib)
+                nc.scalar.activation(out=sg[:], in_=x_t[:, ib, :], func=ACT.Sigmoid)
+                sa = head.tile([P, BATCH], F32, tag="sa", bufs=2, name="sa%d" % ib)
+                nc.vector.scalar_tensor_tensor(out=sa[:], in0=sg[:], scalar=1.0, in1=x_t[:, ib, :], op0=ALU.subtract, op1=ALU.mult)
+                nc.vector.scalar_tensor_tensor(out=sa[:], in0=sa[:], scalar=1.0, in1=sg[:], op0=ALU.subtract, op1=ALU.mult)
+                for hb in range(2):
+                    qb = pq.tile([P, 512], F32, tag="q", name="qb%d_%d" % (ib, hb))
+                    nc.tensor.matmul_mx(
+                        out=qb[:],
+                        lhsT=w_codes[:, BANK_BASE, ib * P : (ib + 1) * P].bitcast(E4),
+                        lhsT_scale=w_scales[:, BANK_BASE, ib * P : (ib + 1) * P],
+                        rhs=go_codes[:, hb * 512 : (hb + 1) * 512].bitcast(E5),
+                        rhs_scale=go_scales[:, hb * 512 : (hb + 1) * 512],
+                        start=True,
+                        stop=True,
+                    )
+                    nc.vector.scalar_tensor_tensor(
+                        out=base_t[:, ib, hb * 512 : (hb + 1) * 512],
+                        in0=sa[:, hb * 512 : (hb + 1) * 512],
+                        scalar=-1.0,
+                        in1=qb[:],
+                        op0=ALU.mult,
+                        op1=ALU.mult,
+                    )
+
+            g12 = head.tile([P, 2048], BF16, name="g12", align_bytes=64)
+            for ib in range(NIB):
+                rv = raws[ib][:].rearrange("p t (i g) -> p i t g", g=NG)
+                for n in range(3):
+                    grp = head.tile([P, 2048], BF16, tag="grp", bufs=3, name="grp%d_%d" % (ib, n), align_bytes=64)
+                    dst = grp[:].rearrange("p (r i t) -> p i t r", r=4, i=P, t=4)
+                    if n < 2:
+                        nc.vector.tensor_copy(out=dst, in_=rv[:, :, :, 4 * n : 4 * n + 4])
+                    else:
+                        nc.scalar.copy(out=dst, in_=rv[:, :, :, 4 * n : 4 * n + 4])
+                    bank = ib * 3 + n
+                    nc.vector.quantize_mx(out=w_codes[:, bank, :].bitcast(E4), scales=w_scales[:, bank, :], in_=grp[:])
+                nc.scalar.copy(
+                    out=g12[:, ib * 512 : (ib + 1) * 512].rearrange("p (i t o) -> p i t o", t=4, o=1),
+                    in_=rv[:, :, :, 12:13],
+                )
+            nc.vector.quantize_mx(out=w_codes[:, BANK_G12, :].bitcast(E4), scales=w_scales[:, BANK_G12, :], in_=g12[:])
+
+            dsel[0] = weights_chunk(0)
+            dsel[1] = weights_chunk(1)
+
+        with tc.tile_pool(name="main", bufs=2) as mainp:
+            for t in range(NT):
+                c = t // 2
+                tl = t % 2
+                npr = mainp.tile([P, 4, IN_F], I32, tag="npr", bufs=2, name="npr%d" % t)
+                for r in range(4):
+                    nc.gpsimd.tensor_scalar(
+                        out=npr[:, r, :], in0=x_sb[:, t, :], scalar1=0.625, scalar2=(8.0 - r) / 4.0 + 0.5, op0=ALU.mult, op1=ALU.add
+                    )
+                ms = {}
+                for bank in range(13):
+                    q = pq.tile([P, 512], F32, tag="q", name="q%d_%d" % (t, bank))
+                    nc.tensor.matmul_mx(
+                        out=q[:],
+                        lhsT=go_codes[:, t * P : (t + 1) * P].bitcast(E5),
+                        lhsT_scale=go_scales[:, t * P : (t + 1) * P],
+                        rhs=w_codes[:, bank, :].bitcast(E4),
+                        rhs_scale=w_scales[:, bank, :],
+                        start=True,
+                        stop=True,
+                    )
+                    m = mainp.tile([P, 512], F32, tag="m", bufs=20, name="m%d_%d" % (t, bank))
+                    if bank == BANK_G12:
+                        nc.vector.scalar_tensor_tensor(out=m[:], in0=npr[:, 0, :], scalar=4.0, in1=q[:], op0=ALU.is_equal, op1=ALU.mult)
+                    else:
+                        ib = bank // 3
+                        n = bank % 3
+                        nc.vector.scalar_tensor_tensor(
+                            out=m[:].rearrange("p (r i) -> p r i", r=4),
+                            in0=npr[:, :, ib * P : (ib + 1) * P],
+                            scalar=float(n + 1),
+                            in1=q[:].rearrange("p (r i) -> p r i", r=4),
+                            op0=ALU.is_equal,
+                            op1=ALU.mult,
+                        )
+                    ms[bank] = m
+                us = []
+                for ib in range(NIB):
+                    sel = psel.tile([P, 512], F32, tag="sel", name="sel%d_%d" % (t, ib))
+                    for r in range(4):
+                        terms = [ms[ib * 3 + n][:, r * P : (r + 1) * P] for n in range(3)]
+                        if r == 0:
+                            terms.append(ms[BANK_G12][:, ib * P : (ib + 1) * P])
+                        for k, term in enumerate(terms):
+                            nc.tensor.matmul(
+                                out=sel[:, r * P : (r + 1) * P],
+                                lhsT=term,
+                                rhs=ident_f[:],
+                                is_transpose=True,
+                                start=(k == 0),
+                                stop=(k == len(terms) - 1),
+                            )
+                    uu = mainp.tile([P, 512], F32, tag="u", bufs=8, name="u%d_%d" % (t, ib))
+                    nc.vector.scalar_tensor_tensor(
+                        out=uu[:].rearrange("p (r b) -> p r b", r=4),
+                        in0=dsel[c][:, :, ib, tl * P : (tl + 1) * P],
+                        scalar=CN,
+                        in1=sel[:].rearrange("p (r b) -> p r b", r=4),
+                        op0=ALU.mult,
+                        op1=ALU.mult,
+                    )
+                    us.append(uu)
+                o = po.tile([P, 512], F32, tag="o", name="o%d" % t)
+                for ib in range(NIB):
+                    terms = [us[ib][:, r * P : (r + 1) * P] for r in range(4)]
+                    terms.append(base_t[:, ib, t * P : (t + 1) * P])
+                    for k, term in enumerate(terms):
+                        nc.tensor.matmul(
+                            out=o[:, ib * P : (ib + 1) * P],
+                            lhsT=term,
+                            rhs=ident_f[:],
+                            is_transpose=True,
+                            start=(k == 0),
+                            stop=(k == len(terms) - 1),
+                        )
+                osb = mainp.tile([P, 512], F32, tag="osb", bufs=2, name="osb%d" % t)
+                nc.scalar.copy(out=osb[:], in_=o[:])
+                nc.sync.dma_start(out=out[t * P : (t + 1) * P, :], in_=osb[:])
+                if tl == 1 and c + 2 < 4:
+                    dsel[c + 2] = weights_chunk(c + 2)

@@ -1,9 +1,7 @@
 from contextlib import ExitStack
 
-import concourse.bass as bass
 import concourse.masks as masks
 import concourse.mybir as mybir
-import concourse.tile as tile
 
 F32 = mybir.dt.float32
 BF16 = mybir.dt.bfloat16
@@ -22,91 +20,203 @@ OUT_F = 512
 NG = 13
 NT = BATCH // P
 NIB = IN_F // P
+NPC = 8
+NGRP = 32
+WCOLS = P * NG
 H = 0.4
 CN = 6.0 * H * H / ((H + 1e-8) * (2.0 * H + 1e-8) * (3.0 * H + 1e-8))
 FLOPS = 2 * BATCH * OUT_F * IN_F * (NG + 1)
-BANK_G12 = 12
-BANK_BASE = 13
+PIN = True
+RG_ON_VECTOR = ((0, 0), (0, 1), (0, 2), (0, 3))
 
 
 def tile_kanlayer_kernel(tc, x, base_w, base_b, spline_w, grad_out, out):
     nc = tc.nc
     with ExitStack() as ctx:
+        if PIN:
+            ctx.enter_context(tc.manual_schedule())
         keep = ctx.enter_context(tc.tile_pool(name="keep", bufs=1))
-        prel = ctx.enter_context(tc.tile_pool(name="prel", bufs=2))
-        pq = ctx.enter_context(tc.psum_pool(name="pq", bufs=3))
+        work = ctx.enter_context(tc.tile_pool(name="work", bufs=2))
+        pq = ctx.enter_context(tc.psum_pool(name="pq", bufs=5))
         psel = ctx.enter_context(tc.psum_pool(name="psel", bufs=2))
         po = ctx.enter_context(tc.psum_pool(name="po", bufs=1))
-        ptp = ctx.enter_context(tc.psum_pool(name="ptp", bufs=2))
 
-        ident_f = keep.tile([P, P], F32, name="ident_f")
-        masks.make_identity(nc, ident_f[:])
         ident_b = keep.tile([P, P], BF16, name="ident_b")
         masks.make_identity(nc, ident_b[:])
+        ident_f = keep.tile([P, P], F32, name="ident_f")
+        masks.make_identity(nc, ident_f[:])
 
-        x_sb = keep.tile([P, NT, IN_F], BF16, name="x_sb")
-        x_t = keep.tile([P, NIB, BATCH], BF16, name="x_t")
+        xc_sb = keep.tile([P, NT, IN_F], BF16, name="xc_sb")
         xc_t = keep.tile([P, NIB, BATCH], BF16, name="xc_t")
         go_codes = keep.tile([P, BATCH], U32, name="go_codes", align_bytes=64)
         go_scales = keep.tile([P, BATCH], U8, name="go_scales", align_bytes=64)
-        w_codes = keep.tile([P, 14, 512], U32, name="w_codes", align_bytes=64)
-        w_scales = keep.tile([P, 14, 512], U8, name="w_scales", align_bytes=64)
-        base_t = keep.tile([P, NIB, BATCH], F32, name="base_t")
+        w_codes = keep.tile([P, NIB, WCOLS], U32, name="w_codes", align_bytes=64)
+        w_scales = keep.tile([P, NIB, WCOLS], U8, name="w_scales", align_bytes=64)
+        b_codes = keep.tile([P, IN_F], U32, name="b_codes", align_bytes=64)
+        b_scales = keep.tile([P, IN_F], U8, name="b_scales", align_bytes=64)
 
-        def weights_chunk(c):
-            src = xc_t[:, :, c * 256 : (c + 1) * 256]
-            fa = prel.tile([P, NIB, 256], F32, tag="fa", name="fa%d" % c)
+        raws = {}
+        grps = {}
+        folds = {}
+        nprs = {}
+        dks = {}
+        sil = {}
+        bts = {}
+        out_v = out.rearrange("(t p) i -> p t i", p=P)
+
+        def load_w(ib):
+            raw = work.tile([P, 4, WCOLS], BF16, tag="raw", bufs=2, name="raw%d" % ib)
+            for u in range(2):
+                nc.sync.dma_start(
+                    out=raw[:, 2 * u : 2 * u + 2, :],
+                    in_=spline_w[256 * u : 256 * u + 256, ib * P : (ib + 1) * P, :].rearrange("(q e) i g -> q e (i g)", e=2),
+                )
+            raws[ib] = raw
+
+        def regroup(ib, n):
+            rv = raws[ib][:].rearrange("p t (i g) -> p i t g", g=NG)
+            if n < 3:
+                grp = work.tile([P, 2048], BF16, tag="grp", bufs=3, name="grp%d_%d" % (ib, n), align_bytes=64)
+                dst = grp[:].rearrange("p (r i t) -> p i t r", r=4, i=P, t=4)
+                src = rv[:, :, :, 4 * n : 4 * n + 4]
+            else:
+                grp = work.tile([P, 512], BF16, tag="grp12", bufs=2, name="grp12_%d" % ib, align_bytes=64)
+                dst = grp[:].rearrange("p (i t o) -> p i t o", t=4, o=1)
+                src = rv[:, :, :, 12:13]
+            if (ib, n) in RG_ON_VECTOR:
+                nc.vector.tensor_copy(out=dst, in_=src)
+            else:
+                nc.scalar.copy(out=dst, in_=src)
+            grps[(ib, n)] = grp
+
+        def quantise_w(ib, n):
+            lo = n * 512
+            hi = lo + (512 if n < 3 else P)
+            nc.vector.quantize_mx(out=w_codes[:, ib, lo:hi].bitcast(E4), scales=w_scales[:, ib, lo:hi], in_=grps[(ib, n)][:])
+
+        def xct(ib):
+            tp = pq.tile([P, BATCH], BF16, tag="q", name="tpx%d" % ib)
+            for t in range(NT):
+                nc.tensor.transpose(out=tp[:, t * P : (t + 1) * P], in_=xc_sb[:, t, ib * P : (ib + 1) * P], identity=ident_b[:])
+            return tp
+
+        def fold(pc):
+            ib = pc // 2
+            hb = pc % 2
+            src = xc_t[:, ib, hb * 512 : (hb + 1) * 512]
+            fa = work.tile([P, 512], F32, tag="fa", name="fa%d" % pc)
             nc.scalar.activation(out=fa[:], in_=src, func=ACT.Abs, scale=2.5)
             nc.scalar.activation(out=fa[:], in_=fa[:], func=ACT.Abs, bias=-4.0)
             nc.scalar.activation(out=fa[:], in_=fa[:], func=ACT.Abs, bias=-2.0)
-            h0 = prel.tile([P, NIB, 256], F32, tag="h0", name="h0%d" % c)
-            nc.scalar.activation(out=h0[:], in_=fa[:], func=ACT.Abs, scale=0.5, bias=-0.5)
-            fe = prel.tile([P, NIB, 256], F32, tag="fe", name="fe%d" % c)
+            al = work.tile([P, 512], F32, tag="al", name="al%d" % pc)
+            nc.scalar.activation(out=al[:], in_=fa[:], func=ACT.Identity, scale=-1.0, bias=1.0)
+            ha = work.tile([P, 512], F32, tag="ha", name="ha%d" % pc)
+            nc.scalar.activation(out=ha[:], in_=fa[:], func=ACT.Abs, scale=0.5, bias=-0.5)
+            fe = work.tile([P, 512], F32, tag="fe", name="fe%d" % pc)
             nc.scalar.activation(out=fe[:], in_=src, func=ACT.Abs, scale=2.5, bias=-1.0)
             nc.scalar.activation(out=fe[:], in_=fe[:], func=ACT.Abs, bias=-4.0)
             nc.scalar.activation(out=fe[:], in_=fe[:], func=ACT.Abs, bias=-2.0)
             nc.scalar.activation(out=fe[:], in_=fe[:], func=ACT.Abs, bias=-2.0)
-            a1 = prel.tile([P, NIB, 256], F32, tag="a1", name="a1%d" % c)
-            nc.scalar.activation(out=a1[:], in_=fe[:], func=ACT.Identity, scale=-1.0, bias=2.0)
-            kk = prel.tile([P, 4, NIB, 256], F32, tag="kk", name="kk%d" % c)
-            nc.vector.scalar_tensor_tensor(out=kk[:, 0], in0=h0[:], scalar=1.5, in1=fa[:], op0=ALU.add, op1=ALU.subtract)
-            nc.vector.scalar_tensor_tensor(out=kk[:, 2], in0=h0[:], scalar=-0.5, in1=fa[:], op0=ALU.add, op1=ALU.add)
-            nc.vector.tensor_tensor(out=kk[:, 1], in0=h0[:], in1=fe[:], op=ALU.subtract)
-            nc.vector.tensor_tensor(out=kk[:, 3], in0=a1[:], in1=h0[:], op=ALU.subtract)
-            nc.vector.scalar_tensor_tensor(out=kk[:, 0], in0=a1[:], scalar=1.0, in1=kk[:, 0], op0=ALU.subtract, op1=ALU.mult)
-            nc.vector.scalar_tensor_tensor(out=kk[:, 2], in0=fe[:], scalar=1.0, in1=kk[:, 2], op0=ALU.subtract, op1=ALU.mult)
-            nc.vector.scalar_tensor_tensor(out=kk[:, 1], in0=fa[:], scalar=1.0, in1=kk[:, 1], op0=ALU.subtract, op1=ALU.mult)
-            nc.vector.scalar_tensor_tensor(out=kk[:, 3], in0=fa[:], scalar=1.0, in1=kk[:, 3], op0=ALU.subtract, op1=ALU.mult)
-            return kk
+            nb = work.tile([P, 512], F32, tag="nb", name="nb%d" % pc)
+            nc.scalar.activation(out=nb[:], in_=fe[:], func=ACT.Identity, scale=-1.0, bias=1.0)
+            folds[pc] = (al, ha, fe, nb)
 
-        dsel = {}
+        def tanh_part(pc):
+            ib = pc // 2
+            hb = pc % 2
+            src = xc_t[:, ib, hb * 512 : (hb + 1) * 512]
+            th = work.tile([P, 512], F32, tag="th", name="th%d" % pc)
+            nc.scalar.activation(out=th[:], in_=src, func=ACT.Tanh, scale=0.5)
+            sn = work.tile([P, 512], F32, tag="sn", name="sn%d" % pc)
+            nc.scalar.activation(out=sn[:], in_=th[:], func=ACT.Identity, scale=-0.5, bias=0.5)
+            nc.scalar.activation(out=th[:], in_=th[:], func=ACT.Identity, scale=0.5, bias=0.5)
+            sil[pc] = (th, sn)
+
+        def plane_index(pc):
+            ib = pc // 2
+            hb = pc % 2
+            npr = work.tile([P, 4, 4, P], I32, tag="npr", bufs=3, name="npr%d" % pc)
+            for r in range(4):
+                nc.gpsimd.tensor_scalar(
+                    out=npr[:, r],
+                    in0=xc_sb[:, 4 * hb : 4 * hb + 4, ib * P : (ib + 1) * P],
+                    scalar1=0.625,
+                    scalar2=(8.0 - r) / 4.0 + 0.5,
+                    op0=ALU.mult,
+                    op1=ALU.add,
+                )
+            nprs[pc] = npr
+
+        def silu_g1(pc, eng):
+            ib = pc // 2
+            hb = pc % 2
+            sn = sil[pc][1]
+            eng.tensor_tensor(out=sn[:], in0=xc_t[:, ib, hb * 512 : (hb + 1) * 512], in1=sn[:], op=ALU.mult)
+
+        def weights_g(pc, eng):
+            al, ha, fe, nb = folds[pc]
+            dk = work.tile([P, 4, 512], F32, tag="dk", bufs=4, name="dk%d" % pc)
+            eng.tensor_tensor(out=dk[:, 0], in0=al[:], in1=ha[:], op=ALU.add)
+            eng.tensor_tensor(out=dk[:, 2], in0=al[:], in1=ha[:], op=ALU.subtract)
+            eng.tensor_tensor(out=dk[:, 3], in0=fe[:], in1=ha[:], op=ALU.add)
+            eng.tensor_tensor(out=dk[:, 1], in0=fe[:], in1=ha[:], op=ALU.subtract)
+            eng.tensor_tensor(out=dk[:, 1], in0=dk[:, 1], in1=al[:], op=ALU.mult)
+            dks[pc] = dk
+
+        def weights_v(pc, which):
+            al, ha, fe, nb = folds[pc]
+            dk = dks[pc]
+            if which == 0:
+                nc.vector.scalar_tensor_tensor(out=dk[:, 0], in0=dk[:, 0], scalar=0.5, in1=nb[:], op0=ALU.add, op1=ALU.mult)
+            elif which == 1:
+                nc.vector.scalar_tensor_tensor(out=dk[:, 2], in0=dk[:, 2], scalar=-0.5, in1=nb[:], op0=ALU.add, op1=ALU.mult)
+            else:
+                nc.vector.scalar_tensor_tensor(out=dk[:, 3], in0=dk[:, 3], scalar=-2.0, in1=al[:], op0=ALU.add, op1=ALU.mult)
+
+        def base_pv(pc):
+            ib = pc // 2
+            hb = pc % 2
+            qb = pq.tile([P, 512], F32, tag="q", name="qb%d" % pc)
+            nc.tensor.matmul_mx(
+                out=qb[:],
+                lhsT=b_codes[:, ib * P : (ib + 1) * P].bitcast(E4),
+                lhsT_scale=b_scales[:, ib * P : (ib + 1) * P],
+                rhs=go_codes[:, hb * 512 : (hb + 1) * 512].bitcast(E5),
+                rhs_scale=go_scales[:, hb * 512 : (hb + 1) * 512],
+                start=True,
+                stop=True,
+            )
+            tb = work.tile([P, 512], F32, tag="tb", name="tb%d" % pc)
+            nc.vector.scalar_tensor_tensor(out=tb[:], in0=sil[pc][1][:], scalar=1.0, in1=qb[:], op0=ALU.add, op1=ALU.mult)
+            bts[pc] = tb
+
+        def base_g(pc, eng):
+            bt = work.tile([P, 512], F32, tag="bt", bufs=3, name="bt%d" % pc)
+            eng.tensor_tensor(out=bt[:], in0=bts[pc][:], in1=sil[pc][0][:], op=ALU.mult)
+            bts[pc] = bt
 
         with tc.tile_pool(name="head", bufs=1) as head:
+            x_sb = head.tile([P, NT, IN_F], BF16, name="x_sb")
+            nc.sync.dma_start(out=x_sb[:], in_=x.rearrange("(t p) i -> p t i", p=P))
             go_sb = head.tile([P, NT, OUT_F], BF16, name="go_sb")
             nc.sync.dma_start(out=go_sb[:], in_=grad_out.rearrange("(t p) o -> p t o", p=P))
-            nc.sync.dma_start(out=x_sb[:], in_=x.rearrange("(t p) i -> p t i", p=P))
+            load_w(0)
             braw = head.tile([P, 4, IN_F], BF16, name="braw")
             for u in range(2):
                 nc.sync.dma_start(
                     out=braw[:, 2 * u : 2 * u + 2, :],
                     in_=base_w[256 * u : 256 * u + 256, :].rearrange("(q e) i -> q e i", e=2),
                 )
-            raws = []
-            for ib in range(NIB):
-                raw = head.tile([P, 4, P * NG], BF16, tag="raw", bufs=2, name="raw%d" % ib)
-                for u in range(2):
-                    nc.sync.dma_start(
-                        out=raw[:, 2 * u : 2 * u + 2, :],
-                        in_=spline_w[256 * u : 256 * u + 256, ib * P : (ib + 1) * P, :].rearrange(
-                            "(q e) i g -> q e (i g)", e=2
-                        ),
-                    )
-                raws.append(raw)
+            load_w(1)
+
+            nc.vector.tensor_scalar(out=xc_sb[:], in0=x_sb[:], scalar1=32.0, scalar2=-32.0, op0=ALU.min, op1=ALU.max)
+            tp0 = xct(0)
+            nc.scalar.copy(out=xc_t[:, 0, :], in_=tp0[:])
 
             ggo = head.tile([P, BATCH * 4], BF16, name="ggo", align_bytes=64)
             ggo_f = ggo[:].bitcast(F32).rearrange("p (b u) -> p b u", u=2)
             for pr in range(NT // 2):
-                gw = ptp.tile([P, 2, 2, P], F32, tag="tp", name="gw%d" % pr)
+                gw = pq.tile([P, 2, 2, P], F32, tag="q", name="gw%d" % pr)
                 for tl in range(2):
                     words = go_sb[:, 2 * pr + tl, :].bitcast(F32)
                     for u in range(2):
@@ -115,157 +225,193 @@ def tile_kanlayer_kernel(tc, x, base_w, base_b, spline_w, grad_out, out):
                     out=ggo_f[:, pr * 256 : (pr + 1) * 256, :].rearrange("p (tl b) u -> p tl b u", tl=2),
                     in_=gw[:].rearrange("p tl u b -> p tl b u"),
                 )
+            tp1 = xct(1)
+            nc.vector.tensor_copy(out=xc_t[:, 1, :], in_=tp1[:])
             for pr in range(NT // 2):
                 nc.vector.quantize_mx(
                     out=go_codes[:, pr * 256 : (pr + 1) * 256].bitcast(E5),
                     scales=go_scales[:, pr * 256 : (pr + 1) * 256],
                     in_=ggo[:, pr * 1024 : (pr + 1) * 1024],
                 )
+            plane_index(0)
+            plane_index(1)
+            fold(0)
+            tanh_part(0)
+            fold(1)
+            tanh_part(1)
 
-            xc_sb = head.tile([P, NT, IN_F], BF16, name="xc_sb")
-            nc.gpsimd.tensor_scalar(out=xc_sb[:], in0=x_sb[:], scalar1=3.25, scalar2=-3.25, op0=ALU.min, op1=ALU.max)
-            for ib in range(NIB):
-                tpx = ptp.tile([P, BATCH], BF16, tag="tp", name="tpx%d" % ib)
-                for t in range(NT):
-                    nc.tensor.transpose(out=tpx[:, t * P : (t + 1) * P], in_=x_sb[:, t, ib * P : (ib + 1) * P], identity=ident_b[:])
-                nc.scalar.copy(out=x_t[:, ib, :], in_=tpx[:])
-            for ib in range(NIB):
-                tpc = ptp.tile([P, BATCH], BF16, tag="tp", name="tpc%d" % ib)
-                for t in range(NT):
-                    nc.tensor.transpose(out=tpc[:, t * P : (t + 1) * P], in_=xc_sb[:, t, ib * P : (ib + 1) * P], identity=ident_b[:])
-                nc.scalar.copy(out=xc_t[:, ib, :], in_=tpc[:])
-
-            bgrp = head.tile([P, 2048], BF16, tag="grp", bufs=3, name="bgrp", align_bytes=64)
+            bgrp = work.tile([P, 2048], BF16, tag="grp", bufs=3, name="bgrp", align_bytes=64)
             nc.vector.tensor_copy(
                 out=bgrp[:].rearrange("p (c i t) -> p c t i", i=4, t=4),
                 in_=braw[:].rearrange("p t (c i) -> p c t i", i=4),
             )
-            nc.vector.quantize_mx(out=w_codes[:, BANK_BASE, :].bitcast(E4), scales=w_scales[:, BANK_BASE, :], in_=bgrp[:])
+            regroup(0, 0)
+            nc.vector.quantize_mx(out=b_codes[:].bitcast(E4), scales=b_scales[:], in_=bgrp[:])
+            regroup(0, 1)
+            quantise_w(0, 0)
+            regroup(0, 2)
+            quantise_w(0, 1)
+            regroup(0, 3)
+            quantise_w(0, 2)
+            quantise_w(0, 3)
+            load_w(2)
 
-            for ib in range(NIB):
-                sg = head.tile([P, BATCH], F32, tag="sg", bufs=2, name="sg%d" % ib)
-                nc.scalar.activation(out=sg[:], in_=x_t[:, ib, :], func=ACT.Sigmoid)
-                sa = head.tile([P, BATCH], F32, tag="sa", bufs=2, name="sa%d" % ib)
-                nc.vector.scalar_tensor_tensor(out=sa[:], in0=sg[:], scalar=1.0, in1=x_t[:, ib, :], op0=ALU.subtract, op1=ALU.mult)
-                nc.vector.scalar_tensor_tensor(out=sa[:], in0=sa[:], scalar=1.0, in1=sg[:], op0=ALU.subtract, op1=ALU.mult)
-                for hb in range(2):
-                    qb = pq.tile([P, 512], F32, tag="q", name="qb%d_%d" % (ib, hb))
-                    nc.tensor.matmul_mx(
-                        out=qb[:],
-                        lhsT=w_codes[:, BANK_BASE, ib * P : (ib + 1) * P].bitcast(E4),
-                        lhsT_scale=w_scales[:, BANK_BASE, ib * P : (ib + 1) * P],
-                        rhs=go_codes[:, hb * 512 : (hb + 1) * 512].bitcast(E5),
-                        rhs_scale=go_scales[:, hb * 512 : (hb + 1) * 512],
-                        start=True,
-                        stop=True,
-                    )
-                    nc.vector.scalar_tensor_tensor(
-                        out=base_t[:, ib, hb * 512 : (hb + 1) * 512],
-                        in0=sa[:, hb * 512 : (hb + 1) * 512],
-                        scalar=-1.0,
-                        in1=qb[:],
-                        op0=ALU.mult,
-                        op1=ALU.mult,
-                    )
+            regroup(1, 0)
+            regroup(1, 1)
+            weights_g(1, nc.gpsimd)
+            silu_g1(1, nc.gpsimd)
 
-            g12 = head.tile([P, 2048], BF16, name="g12", align_bytes=64)
-            for ib in range(NIB):
-                rv = raws[ib][:].rearrange("p t (i g) -> p i t g", g=NG)
-                for n in range(3):
-                    grp = head.tile([P, 2048], BF16, tag="grp", bufs=3, name="grp%d_%d" % (ib, n), align_bytes=64)
-                    dst = grp[:].rearrange("p (r i t) -> p i t r", r=4, i=P, t=4)
-                    if n < 2:
-                        nc.vector.tensor_copy(out=dst, in_=rv[:, :, :, 4 * n : 4 * n + 4])
-                    else:
-                        nc.scalar.copy(out=dst, in_=rv[:, :, :, 4 * n : 4 * n + 4])
-                    bank = ib * 3 + n
-                    nc.vector.quantize_mx(out=w_codes[:, bank, :].bitcast(E4), scales=w_scales[:, bank, :], in_=grp[:])
-                nc.scalar.copy(
-                    out=g12[:, ib * 512 : (ib + 1) * 512].rearrange("p (i t o) -> p i t o", t=4, o=1),
-                    in_=rv[:, :, :, 12:13],
-                )
-            nc.vector.quantize_mx(out=w_codes[:, BANK_G12, :].bitcast(E4), scales=w_scales[:, BANK_G12, :], in_=g12[:])
+        with tc.tile_pool(name="main", bufs=3) as mainp:
+            ms = {}
+            sels = {}
+            us = {}
+            os_ = {}
 
-            dsel[0] = weights_chunk(0)
-            dsel[1] = weights_chunk(1)
-
-        with tc.tile_pool(name="main", bufs=2) as mainp:
-            for t in range(NT):
-                c = t // 2
-                tl = t % 2
-                npr = mainp.tile([P, 4, IN_F], I32, tag="npr", bufs=2, name="npr%d" % t)
-                for r in range(4):
-                    nc.gpsimd.tensor_scalar(
-                        out=npr[:, r, :], in0=x_sb[:, t, :], scalar1=0.625, scalar2=(8.0 - r) / 4.0 + 0.5, op0=ALU.mult, op1=ALU.add
-                    )
-                ms = {}
-                for bank in range(13):
-                    q = pq.tile([P, 512], F32, tag="q", name="q%d_%d" % (t, bank))
+            def mx_and_mask(k):
+                pc = k // 4
+                tq = k % 4
+                ib = pc // 2
+                t = 4 * (pc % 2) + tq
+                qs = []
+                for n in range(4):
+                    lo = n * 512 if n < 3 else WCOLS - 512
+                    q = pq.tile([P, 512], F32, tag="q", name="q%d_%d" % (k, n))
                     nc.tensor.matmul_mx(
                         out=q[:],
                         lhsT=go_codes[:, t * P : (t + 1) * P].bitcast(E5),
                         lhsT_scale=go_scales[:, t * P : (t + 1) * P],
-                        rhs=w_codes[:, bank, :].bitcast(E4),
-                        rhs_scale=w_scales[:, bank, :],
+                        rhs=w_codes[:, ib, lo : lo + 512].bitcast(E4),
+                        rhs_scale=w_scales[:, ib, lo : lo + 512],
                         start=True,
                         stop=True,
                     )
-                    m = mainp.tile([P, 512], F32, tag="m", bufs=20, name="m%d_%d" % (t, bank))
-                    if bank == BANK_G12:
-                        nc.vector.scalar_tensor_tensor(out=m[:], in0=npr[:, 0, :], scalar=4.0, in1=q[:], op0=ALU.is_equal, op1=ALU.mult)
-                    else:
-                        ib = bank // 3
-                        n = bank % 3
-                        nc.vector.scalar_tensor_tensor(
-                            out=m[:].rearrange("p (r i) -> p r i", r=4),
-                            in0=npr[:, :, ib * P : (ib + 1) * P],
-                            scalar=float(n + 1),
-                            in1=q[:].rearrange("p (r i) -> p r i", r=4),
-                            op0=ALU.is_equal,
-                            op1=ALU.mult,
-                        )
-                    ms[bank] = m
-                us = []
-                for ib in range(NIB):
-                    sel = psel.tile([P, 512], F32, tag="sel", name="sel%d_%d" % (t, ib))
-                    for r in range(4):
-                        terms = [ms[ib * 3 + n][:, r * P : (r + 1) * P] for n in range(3)]
-                        if r == 0:
-                            terms.append(ms[BANK_G12][:, ib * P : (ib + 1) * P])
-                        for k, term in enumerate(terms):
-                            nc.tensor.matmul(
-                                out=sel[:, r * P : (r + 1) * P],
-                                lhsT=term,
-                                rhs=ident_f[:],
-                                is_transpose=True,
-                                start=(k == 0),
-                                stop=(k == len(terms) - 1),
-                            )
-                    uu = mainp.tile([P, 512], F32, tag="u", bufs=8, name="u%d_%d" % (t, ib))
+                    qs.append(q)
+                npr = nprs[pc]
+                tiles = []
+                for n in range(3):
+                    m = mainp.tile([P, 512], F32, tag="m", bufs=9, name="m%d_%d" % (k, n))
                     nc.vector.scalar_tensor_tensor(
-                        out=uu[:].rearrange("p (r b) -> p r b", r=4),
-                        in0=dsel[c][:, :, ib, tl * P : (tl + 1) * P],
-                        scalar=CN,
-                        in1=sel[:].rearrange("p (r b) -> p r b", r=4),
-                        op0=ALU.mult,
+                        out=m[:].rearrange("p (r i) -> p r i", r=4),
+                        in0=npr[:, :, tq, :],
+                        scalar=float(n + 1),
+                        in1=qs[n][:].rearrange("p (r i) -> p r i", r=4),
+                        op0=ALU.is_equal,
                         op1=ALU.mult,
                     )
-                    us.append(uu)
-                o = po.tile([P, 512], F32, tag="o", name="o%d" % t)
-                for ib in range(NIB):
-                    terms = [us[ib][:, r * P : (r + 1) * P] for r in range(4)]
-                    terms.append(base_t[:, ib, t * P : (t + 1) * P])
-                    for k, term in enumerate(terms):
+                    tiles.append(m)
+                m12 = mainp.tile([P, P], F32, tag="m12", bufs=3, name="m12_%d" % k)
+                nc.vector.scalar_tensor_tensor(
+                    out=m12[:], in0=npr[:, 0, tq, :], scalar=4.0, in1=qs[3][:, 384:512], op0=ALU.is_equal, op1=ALU.mult
+                )
+                tiles.append(m12)
+                ms[k] = tiles
+
+            def class_sums(k):
+                sel = psel.tile([P, 512], F32, tag="sel", name="sel%d" % k)
+                for r in range(4):
+                    terms = [ms[k][n][:, r * P : (r + 1) * P] for n in range(3)]
+                    if r == 0:
+                        terms.append(ms[k][3][:])
+                    for j, term in enumerate(terms):
                         nc.tensor.matmul(
-                            out=o[:, ib * P : (ib + 1) * P],
+                            out=sel[:, r * P : (r + 1) * P],
                             lhsT=term,
                             rhs=ident_f[:],
                             is_transpose=True,
-                            start=(k == 0),
-                            stop=(k == len(terms) - 1),
+                            start=(j == 0),
+                            stop=(j == len(terms) - 1),
                         )
-                osb = mainp.tile([P, 512], F32, tag="osb", bufs=2, name="osb%d" % t)
-                nc.scalar.copy(out=osb[:], in_=o[:])
-                nc.sync.dma_start(out=out[t * P : (t + 1) * P, :], in_=osb[:])
-                if tl == 1 and c + 2 < 4:
-                    dsel[c + 2] = weights_chunk(c + 2)
+                sels[k] = sel
+
+            def weigh(k):
+                pc = k // 4
+                tq = k % 4
+                uu = mainp.tile([P, 512], F32, tag="u", bufs=3, name="u%d" % k)
+                nc.vector.scalar_tensor_tensor(
+                    out=uu[:].rearrange("p (r b) -> p r b", r=4),
+                    in0=dks[pc][:, :, tq * P : (tq + 1) * P],
+                    scalar=CN,
+                    in1=sels[k][:].rearrange("p (r b) -> p r b", r=4),
+                    op0=ALU.mult,
+                    op1=ALU.mult,
+                )
+                us[k] = uu
+
+            def final_sums(k):
+                pc = k // 4
+                tq = k % 4
+                if tq == 0:
+                    os_[pc] = po.tile([P, 512], F32, tag="o", name="o%d" % pc)
+                o = os_[pc]
+                terms = [us[k][:, r * P : (r + 1) * P] for r in range(4)]
+                terms.append(bts[pc][:, tq * P : (tq + 1) * P])
+                for j, term in enumerate(terms):
+                    nc.tensor.matmul(
+                        out=o[:, tq * P : (tq + 1) * P],
+                        lhsT=term,
+                        rhs=ident_f[:],
+                        is_transpose=True,
+                        start=(j == 0),
+                        stop=(j == len(terms) - 1),
+                    )
+
+            def store(pc):
+                ib = pc // 2
+                hb = pc % 2
+                osb = mainp.tile([P, 512], F32, tag="osb", bufs=2, name="osb%d" % pc)
+                nc.scalar.copy(out=osb[:], in_=os_[pc][:])
+                nc.sync.dma_start(
+                    out=out_v[:, 4 * hb : 4 * hb + 4, ib * P : (ib + 1) * P],
+                    in_=osb[:].rearrange("p (t i) -> p t i", t=4),
+                )
+
+            for j in range(NGRP + 2):
+                pc = j // 4
+                i = j % 4
+                nxt = pc + 1
+                live = j < NGRP
+                if live:
+                    mx_and_mask(j)
+                if 0 <= j - 1 < NGRP:
+                    class_sums(j - 1)
+                if j == 1:
+                    weights_g(0, nc.vector)
+                    for which in range(3):
+                        weights_v(0, which)
+                    silu_g1(0, nc.vector)
+                    base_pv(0)
+                    base_g(0, nc.vector)
+                if live and nxt < NPC and i >= 1:
+                    weights_v(nxt, i - 1)
+                if live and pc % 2 == 1 and pc // 2 + 1 < NIB:
+                    quantise_w(pc // 2 + 1, i)
+                if 0 <= j - 1 < NGRP:
+                    weigh(j - 1)
+                if 0 <= j - 2 < NGRP:
+                    final_sums(j - 2)
+                    if (j - 2) % 4 == 3:
+                        store((j - 2) // 4)
+                if live and i == 1:
+                    if pc + 2 < NPC:
+                        fold(pc + 2)
+                        tanh_part(pc + 2)
+                    if pc % 2 == 1 and (pc + 3) // 2 < NIB:
+                        regroup((pc + 3) // 2, 0)
+                        regroup((pc + 3) // 2, 1)
+                    if pc % 2 == 0 and (pc + 2) // 2 < NIB:
+                        regroup((pc + 2) // 2, 2)
+                        regroup((pc + 2) // 2, 3)
+                        if (pc + 2) // 2 + 2 < NIB:
+                            load_w((pc + 2) // 2 + 2)
+                if live and i == 2 and pc + 2 < NPC:
+                    plane_index(pc + 2)
+                    weights_g(pc + 2, nc.gpsimd)
+                    silu_g1(pc + 2, nc.gpsimd)
+                if live and i == 3:
+                    if j == 3 or j == 11:
+                        ibx = 2 if j == 3 else 3
+                        tpx = xct(ibx)
+                        nc.vector.tensor_copy(out=xc_t[:, ibx, :], in_=tpx[:])
+                    if nxt < NPC:
+                        base_pv(nxt)
+                        base_g(nxt, nc.gpsimd)

@@ -267,13 +267,16 @@ def tile_kanlayer_kernel(tc, x, base_w, base_b, spline_w, grad_out, out):
             us = {}
             os_ = {}
 
-            def mx_and_mask(k):
+            def mx_and_mask(k, half):
                 pc = k // 4
                 tq = k % 4
                 ib = pc // 2
                 t = 4 * (pc % 2) + tq
+                npr = nprs[pc]
+                if half == 0:
+                    ms[k] = []
                 qs = []
-                for n in range(4):
+                for n in (2 * half, 2 * half + 1):
                     lo = n * 512 if n < 3 else WCOLS - 512
                     q = pq.tile([P, 512], F32, tag="q", name="q%d_%d" % (k, n))
                     nc.tensor.matmul_mx(
@@ -286,29 +289,30 @@ def tile_kanlayer_kernel(tc, x, base_w, base_b, spline_w, grad_out, out):
                         stop=True,
                     )
                     qs.append(q)
-                npr = nprs[pc]
-                tiles = []
-                for n in range(3):
-                    m = mainp.tile([P, 512], F32, tag="m", bufs=9, name="m%d_%d" % (k, n))
-                    nc.vector.scalar_tensor_tensor(
-                        out=m[:].rearrange("p (r i) -> p r i", r=4),
-                        in0=npr[:, :, tq, :],
-                        scalar=float(n + 1),
-                        in1=qs[n][:].rearrange("p (r i) -> p r i", r=4),
-                        op0=ALU.is_equal,
-                        op1=ALU.mult,
-                    )
-                    tiles.append(m)
-                m12 = mainp.tile([P, P], F32, tag="m12", bufs=3, name="m12_%d" % k)
-                nc.vector.scalar_tensor_tensor(
-                    out=m12[:], in0=npr[:, 0, tq, :], scalar=4.0, in1=qs[3][:, 384:512], op0=ALU.is_equal, op1=ALU.mult
-                )
-                tiles.append(m12)
-                ms[k] = tiles
+                for n in (2 * half, 2 * half + 1):
+                    q = qs[n - 2 * half]
+                    if n < 3:
+                        m = mainp.tile([P, 512], F32, tag="m", bufs=9, name="m%d_%d" % (k, n))
+                        nc.vector.scalar_tensor_tensor(
+                            out=m[:].rearrange("p (r i) -> p r i", r=4),
+                            in0=npr[:, :, tq, :],
+                            scalar=float(n + 1),
+                            in1=q[:].rearrange("p (r i) -> p r i", r=4),
+                            op0=ALU.is_equal,
+                            op1=ALU.mult,
+                        )
+                    else:
+                        m = mainp.tile([P, P], F32, tag="m12", bufs=3, name="m12_%d" % k)
+                        nc.vector.scalar_tensor_tensor(
+                            out=m[:], in0=npr[:, 0, tq, :], scalar=4.0, in1=q[:, 384:512], op0=ALU.is_equal, op1=ALU.mult
+                        )
+                    ms[k].append(m)
 
-            def class_sums(k):
-                sel = psel.tile([P, 512], F32, tag="sel", name="sel%d" % k)
-                for r in range(4):
+            def class_sums(k, half):
+                if half == 0:
+                    sels[k] = psel.tile([P, 512], F32, tag="sel", name="sel%d" % k)
+                sel = sels[k]
+                for r in (2 * half, 2 * half + 1):
                     terms = [ms[k][n][:, r * P : (r + 1) * P] for n in range(3)]
                     if r == 0:
                         terms.append(ms[k][3][:])
@@ -321,7 +325,6 @@ def tile_kanlayer_kernel(tc, x, base_w, base_b, spline_w, grad_out, out):
                             start=(j == 0),
                             stop=(j == len(terms) - 1),
                         )
-                sels[k] = sel
 
             def weigh(k):
                 pc = k // 4
@@ -371,22 +374,26 @@ def tile_kanlayer_kernel(tc, x, base_w, base_b, spline_w, grad_out, out):
                 nxt = pc + 1
                 live = j < NGRP
                 if live:
-                    mx_and_mask(j)
+                    mx_and_mask(j, 0)
                 if 0 <= j - 1 < NGRP:
-                    class_sums(j - 1)
-                if j == 1:
+                    class_sums(j - 1, 0)
+                if j == 2:
                     weights_g(0, nc.vector)
                     for which in range(3):
                         weights_v(0, which)
                     silu_g1(0, nc.vector)
                     base_pv(0)
                     base_g(0, nc.vector)
+                if 0 <= j - 2 < NGRP:
+                    weigh(j - 2)
+                if live:
+                    mx_and_mask(j, 1)
+                if 0 <= j - 1 < NGRP:
+                    class_sums(j - 1, 1)
                 if live and nxt < NPC and i >= 1:
                     weights_v(nxt, i - 1)
                 if live and pc % 2 == 1 and pc // 2 + 1 < NIB:
                     quantise_w(pc // 2 + 1, i)
-                if 0 <= j - 1 < NGRP:
-                    weigh(j - 1)
                 if 0 <= j - 2 < NGRP:
                     final_sums(j - 2)
                     if (j - 2) % 4 == 3:

@@ -108,8 +108,12 @@ def tile_kanlayer_kernel(tc, x, base_w, base_b, spline_w, grad_out, out):
             nc.scalar.activation(out=fa[:], in_=src, func=ACT.Abs, scale=2.5)
             nc.scalar.activation(out=fa[:], in_=fa[:], func=ACT.Abs, bias=-4.0)
             nc.scalar.activation(out=fa[:], in_=fa[:], func=ACT.Abs, bias=-2.0)
-            al = work.tile([P, 512], F32, tag="al", name="al%d" % pc)
+            al = work.tile([P, 512], F32, tag="al", bufs=3, name="al%d" % pc)
             nc.scalar.activation(out=al[:], in_=fa[:], func=ACT.Identity, scale=-1.0, bias=1.0)
+            alp = work.tile([P, 512], F32, tag="alp", name="alp%d" % pc)
+            nc.scalar.activation(out=alp[:], in_=fa[:], func=ACT.Identity, scale=-1.0, bias=1.5)
+            alm = work.tile([P, 512], F32, tag="alm", name="alm%d" % pc)
+            nc.scalar.activation(out=alm[:], in_=fa[:], func=ACT.Identity, scale=-1.0, bias=0.5)
             ha = work.tile([P, 512], F32, tag="ha", name="ha%d" % pc)
             nc.scalar.activation(out=ha[:], in_=fa[:], func=ACT.Abs, scale=0.5, bias=-0.5)
             fe = work.tile([P, 512], F32, tag="fe", name="fe%d" % pc)
@@ -119,7 +123,7 @@ def tile_kanlayer_kernel(tc, x, base_w, base_b, spline_w, grad_out, out):
             nc.scalar.activation(out=fe[:], in_=fe[:], func=ACT.Abs, bias=-2.0)
             nb = work.tile([P, 512], F32, tag="nb", name="nb%d" % pc)
             nc.scalar.activation(out=nb[:], in_=fe[:], func=ACT.Identity, scale=-1.0, bias=1.0)
-            folds[pc] = (al, ha, fe, nb)
+            folds[pc] = (al, ha, fe, nb, alp, alm)
 
         def tanh_part(pc):
             ib = pc // 2
@@ -127,7 +131,7 @@ def tile_kanlayer_kernel(tc, x, base_w, base_b, spline_w, grad_out, out):
             src = xc_t[:, ib, hb * 512 : (hb + 1) * 512]
             th = work.tile([P, 512], F32, tag="th", name="th%d" % pc)
             nc.scalar.activation(out=th[:], in_=src, func=ACT.Tanh, scale=0.5)
-            sn = work.tile([P, 512], F32, tag="sn", name="sn%d" % pc)
+            sn = work.tile([P, 512], F32, tag="sn", bufs=3, name="sn%d" % pc)
             nc.scalar.activation(out=sn[:], in_=th[:], func=ACT.Identity, scale=-0.5, bias=0.5)
             nc.scalar.activation(out=th[:], in_=th[:], func=ACT.Identity, scale=0.5, bias=0.5)
             sil[pc] = (th, sn)
@@ -154,24 +158,29 @@ def tile_kanlayer_kernel(tc, x, base_w, base_b, spline_w, grad_out, out):
             eng.tensor_tensor(out=sn[:], in0=xc_t[:, ib, hb * 512 : (hb + 1) * 512], in1=sn[:], op=ALU.mult)
 
         def weights_g(pc, eng):
-            al, ha, fe, nb = folds[pc]
+            al, ha, fe, nb, alp, alm = folds[pc]
             dk = work.tile([P, 4, 512], F32, tag="dk", bufs=4, name="dk%d" % pc)
-            eng.tensor_tensor(out=dk[:, 0], in0=al[:], in1=ha[:], op=ALU.add)
-            eng.tensor_tensor(out=dk[:, 2], in0=al[:], in1=ha[:], op=ALU.subtract)
             eng.tensor_tensor(out=dk[:, 3], in0=fe[:], in1=ha[:], op=ALU.add)
+            eng.tensor_tensor(out=dk[:, 0], in0=alp[:], in1=ha[:], op=ALU.add)
+            eng.tensor_tensor(out=dk[:, 2], in0=alm[:], in1=ha[:], op=ALU.subtract)
             eng.tensor_tensor(out=dk[:, 1], in0=fe[:], in1=ha[:], op=ALU.subtract)
+            eng.tensor_tensor(out=dk[:, 0], in0=dk[:, 0], in1=nb[:], op=ALU.mult)
+            eng.tensor_tensor(out=dk[:, 2], in0=dk[:, 2], in1=nb[:], op=ALU.mult)
             eng.tensor_tensor(out=dk[:, 1], in0=dk[:, 1], in1=al[:], op=ALU.mult)
             dks[pc] = dk
 
-        def weights_v(pc, which):
-            al, ha, fe, nb = folds[pc]
+        def weights_v(pc):
+            al = folds[pc][0]
             dk = dks[pc]
-            if which == 0:
-                nc.vector.scalar_tensor_tensor(out=dk[:, 0], in0=dk[:, 0], scalar=0.5, in1=nb[:], op0=ALU.add, op1=ALU.mult)
-            elif which == 1:
-                nc.vector.scalar_tensor_tensor(out=dk[:, 2], in0=dk[:, 2], scalar=-0.5, in1=nb[:], op0=ALU.add, op1=ALU.mult)
-            else:
-                nc.vector.scalar_tensor_tensor(out=dk[:, 3], in0=dk[:, 3], scalar=-2.0, in1=al[:], op0=ALU.add, op1=ALU.mult)
+            nc.vector.scalar_tensor_tensor(out=dk[:, 3], in0=dk[:, 3], scalar=-2.0, in1=al[:], op0=ALU.add, op1=ALU.mult)
+
+        def silu_s2(pc):
+            sn = sil[pc][1]
+            nc.scalar.activation(out=sn[:], in_=sn[:], func=ACT.Identity, scale=1.0, bias=1.0)
+
+        def silu_g3(pc, eng):
+            th, sn = sil[pc]
+            eng.tensor_tensor(out=sn[:], in0=sn[:], in1=th[:], op=ALU.mult)
 
         def base_pv(pc):
             ib = pc // 2
@@ -186,13 +195,8 @@ def tile_kanlayer_kernel(tc, x, base_w, base_b, spline_w, grad_out, out):
                 start=True,
                 stop=True,
             )
-            tb = work.tile([P, 512], F32, tag="tb", name="tb%d" % pc)
-            nc.vector.scalar_tensor_tensor(out=tb[:], in0=sil[pc][1][:], scalar=1.0, in1=qb[:], op0=ALU.add, op1=ALU.mult)
-            bts[pc] = tb
-
-        def base_g(pc, eng):
             bt = work.tile([P, 512], F32, tag="bt", bufs=3, name="bt%d" % pc)
-            eng.tensor_tensor(out=bt[:], in0=bts[pc][:], in1=sil[pc][0][:], op=ALU.mult)
+            nc.vector.tensor_tensor(out=bt[:], in0=sil[pc][1][:], in1=qb[:], op=ALU.mult)
             bts[pc] = bt
 
         with tc.tile_pool(name="head", bufs=1) as head:
@@ -235,10 +239,10 @@ def tile_kanlayer_kernel(tc, x, base_w, base_b, spline_w, grad_out, out):
                 )
             plane_index(0)
             plane_index(1)
-            fold(0)
             tanh_part(0)
-            fold(1)
+            fold(0)
             tanh_part(1)
+            fold(1)
 
             bgrp = work.tile([P, 2048], BF16, tag="grp", bufs=3, name="bgrp", align_bytes=64)
             nc.vector.tensor_copy(
@@ -258,8 +262,10 @@ def tile_kanlayer_kernel(tc, x, base_w, base_b, spline_w, grad_out, out):
 
             regroup(1, 0)
             regroup(1, 1)
-            weights_g(1, nc.gpsimd)
             silu_g1(1, nc.gpsimd)
+            weights_g(1, nc.gpsimd)
+            silu_s2(1)
+            silu_g3(1, nc.gpsimd)
 
         with tc.tile_pool(name="main", bufs=3) as mainp:
             ms = {}
@@ -371,27 +377,25 @@ def tile_kanlayer_kernel(tc, x, base_w, base_b, spline_w, grad_out, out):
             for j in range(NGRP + 2):
                 pc = j // 4
                 i = j % 4
-                nxt = pc + 1
                 live = j < NGRP
                 if live:
                     mx_and_mask(j, 0)
                 if 0 <= j - 1 < NGRP:
                     class_sums(j - 1, 0)
-                if j == 2:
-                    weights_g(0, nc.vector)
-                    for which in range(3):
-                        weights_v(0, which)
-                    silu_g1(0, nc.vector)
-                    base_pv(0)
-                    base_g(0, nc.vector)
                 if 0 <= j - 2 < NGRP:
                     weigh(j - 2)
                 if live:
                     mx_and_mask(j, 1)
                 if 0 <= j - 1 < NGRP:
                     class_sums(j - 1, 1)
-                if live and nxt < NPC and i >= 1:
-                    weights_v(nxt, i - 1)
+                if j == 1:
+                    weights_g(0, nc.vector)
+                    silu_g1(0, nc.vector)
+                    nc.vector.scalar_tensor_tensor(
+                        out=sil[0][1][:], in0=sil[0][1][:], scalar=1.0, in1=sil[0][0][:], op0=ALU.add, op1=ALU.mult
+                    )
+                if live and i == 1:
+                    weights_v(pc)
                 if live and pc % 2 == 1 and pc // 2 + 1 < NIB:
                     quantise_w(pc // 2 + 1, i)
                 if 0 <= j - 2 < NGRP:
@@ -399,9 +403,10 @@ def tile_kanlayer_kernel(tc, x, base_w, base_b, spline_w, grad_out, out):
                     if (j - 2) % 4 == 3:
                         store((j - 2) // 4)
                 if live and i == 1:
+                    base_pv(pc)
                     if pc + 2 < NPC:
-                        fold(pc + 2)
                         tanh_part(pc + 2)
+                        fold(pc + 2)
                     if pc % 2 == 1 and (pc + 3) // 2 < NIB:
                         regroup((pc + 3) // 2, 0)
                         regroup((pc + 3) // 2, 1)
@@ -411,14 +416,12 @@ def tile_kanlayer_kernel(tc, x, base_w, base_b, spline_w, grad_out, out):
                         if (pc + 2) // 2 + 2 < NIB:
                             load_w((pc + 2) // 2 + 2)
                 if live and i == 2 and pc + 2 < NPC:
+                    silu_g1(pc + 2, nc.gpsimd)
                     plane_index(pc + 2)
                     weights_g(pc + 2, nc.gpsimd)
-                    silu_g1(pc + 2, nc.gpsimd)
-                if live and i == 3:
-                    if j == 3 or j == 11:
-                        ibx = 2 if j == 3 else 3
-                        tpx = xct(ibx)
-                        nc.vector.tensor_copy(out=xc_t[:, ibx, :], in_=tpx[:])
-                    if nxt < NPC:
-                        base_pv(nxt)
-                        base_g(nxt, nc.gpsimd)
+                    silu_s2(pc + 2)
+                    silu_g3(pc + 2, nc.gpsimd)
+                if j == 3 or j == 11:
+                    ibx = 2 if j == 3 else 3
+                    tpx = xct(ibx)
+                    nc.vector.tensor_copy(out=xc_t[:, ibx, :], in_=tpx[:])

@@ -77,7 +77,7 @@ def tile_kanlayer_kernel(tc, x, base_w, base_b, spline_w, grad_out, out):
             rv = raws[ib][:].rearrange("p t (i g) -> p i t g", g=NG)
             if n < 3:
                 grp = work.tile([P, 2048], BF16, tag="grp", bufs=3, name="grp%d_%d" % (ib, n), align_bytes=64)
-                dst = grp[:].rearrange("p (r i t) -> p i t r", r=4, i=P, t=4)
+                dst = grp[:].rearrange("p (i r t) -> p i t r", r=4, i=P, t=4)
                 src = rv[:, :, :, 4 * n : 4 * n + 4]
             else:
                 grp = work.tile([P, 512], BF16, tag="grp12", bufs=2, name="grp12_%d" % ib, align_bytes=64)
@@ -303,7 +303,7 @@ def tile_kanlayer_kernel(tc, x, base_w, base_b, spline_w, grad_out, out):
                             out=m[:].rearrange("p (r i) -> p r i", r=4),
                             in0=npr[:, :, tq, :],
                             scalar=float(n + 1),
-                            in1=q[:].rearrange("p (r i) -> p r i", r=4),
+                            in1=q[:].rearrange("p (i r) -> p r i", r=4),
                             op0=ALU.is_equal,
                             op1=ALU.mult,
                         )

@@ -77,7 +77,7 @@ def tile_kanlayer_kernel(tc, x, base_w, base_b, spline_w, grad_out, out):
             rv = raws[ib][:].rearrange("p t (i g) -> p i t g", g=NG)
             if n < 3:
                 grp = work.tile([P, 2048], BF16, tag="grp", bufs=3, name="grp%d_%d" % (ib, n), align_bytes=64)
-                dst = grp[:].rearrange("p (i r t) -> p i t r", r=4, i=P, t=4)
+                dst = grp[:].rearrange("p (r i t) -> p i t r", r=4, i=P, t=4)
                 src = rv[:, :, :, 4 * n : 4 * n + 4]
             else:
                 grp = work.tile([P, 512], BF16, tag="grp12", bufs=2, name="grp12_%d" % ib, align_bytes=64)
@@ -108,12 +108,8 @@ def tile_kanlayer_kernel(tc, x, base_w, base_b, spline_w, grad_out, out):
             nc.scalar.activation(out=fa[:], in_=src, func=ACT.Abs, scale=2.5)
             nc.scalar.activation(out=fa[:], in_=fa[:], func=ACT.Abs, bias=-4.0)
             nc.scalar.activation(out=fa[:], in_=fa[:], func=ACT.Abs, bias=-2.0)
-            al = work.tile([P, 512], F32, tag="al", bufs=3, name="al%d" % pc)
+            al = work.tile([P, 512], F32, tag="al", name="al%d" % pc)
             nc.scalar.activation(out=al[:], in_=fa[:], func=ACT.Identity, scale=-1.0, bias=1.0)
-            alp = work.tile([P, 512], F32, tag="alp", name="alp%d" % pc)
-            nc.scalar.activation(out=alp[:], in_=fa[:], func=ACT.Identity, scale=-1.0, bias=1.5)
-            alm = work.tile([P, 512], F32, tag="alm", name="alm%d" % pc)
-            nc.scalar.activation(out=alm[:], in_=fa[:], func=ACT.Identity, scale=-1.0, bias=0.5)
             ha = work.tile([P, 512], F32, tag="ha", name="ha%d" % pc)
             nc.scalar.activation(out=ha[:], in_=fa[:], func=ACT.Abs, scale=0.5, bias=-0.5)
             fe = work.tile([P, 512], F32, tag="fe", name="fe%d" % pc)
@@ -123,7 +119,7 @@ def tile_kanlayer_kernel(tc, x, base_w, base_b, spline_w, grad_out, out):
             nc.scalar.activation(out=fe[:], in_=fe[:], func=ACT.Abs, bias=-2.0)
             nb = work.tile([P, 512], F32, tag="nb", name="nb%d" % pc)
             nc.scalar.activation(out=nb[:], in_=fe[:], func=ACT.Identity, scale=-1.0, bias=1.0)
-            folds[pc] = (al, ha, fe, nb, alp, alm)
+            folds[pc] = (al, ha, fe, nb)
 
         def tanh_part(pc):
             ib = pc // 2
@@ -131,7 +127,7 @@ def tile_kanlayer_kernel(tc, x, base_w, base_b, spline_w, grad_out, out):
             src = xc_t[:, ib, hb * 512 : (hb + 1) * 512]
             th = work.tile([P, 512], F32, tag="th", name="th%d" % pc)
             nc.scalar.activation(out=th[:], in_=src, func=ACT.Tanh, scale=0.5)
-            sn = work.tile([P, 512], F32, tag="sn", bufs=3, name="sn%d" % pc)
+            sn = work.tile([P, 512], F32, tag="sn", name="sn%d" % pc)
             nc.scalar.activation(out=sn[:], in_=th[:], func=ACT.Identity, scale=-0.5, bias=0.5)
             nc.scalar.activation(out=th[:], in_=th[:], func=ACT.Identity, scale=0.5, bias=0.5)
             sil[pc] = (th, sn)
@@ -158,29 +154,24 @@ def tile_kanlayer_kernel(tc, x, base_w, base_b, spline_w, grad_out, out):
             eng.tensor_tensor(out=sn[:], in0=xc_t[:, ib, hb * 512 : (hb + 1) * 512], in1=sn[:], op=ALU.mult)
 
         def weights_g(pc, eng):
-            al, ha, fe, nb, alp, alm = folds[pc]
+            al, ha, fe, nb = folds[pc]
             dk = work.tile([P, 4, 512], F32, tag="dk", bufs=4, name="dk%d" % pc)
+            eng.tensor_tensor(out=dk[:, 0], in0=al[:], in1=ha[:], op=ALU.add)
+            eng.tensor_tensor(out=dk[:, 2], in0=al[:], in1=ha[:], op=ALU.subtract)
             eng.tensor_tensor(out=dk[:, 3], in0=fe[:], in1=ha[:], op=ALU.add)
-            eng.tensor_tensor(out=dk[:, 0], in0=alp[:], in1=ha[:], op=ALU.add)
-            eng.tensor_tensor(out=dk[:, 2], in0=alm[:], in1=ha[:], op=ALU.subtract)
             eng.tensor_tensor(out=dk[:, 1], in0=fe[:], in1=ha[:], op=ALU.subtract)
-            eng.tensor_tensor(out=dk[:, 0], in0=dk[:, 0], in1=nb[:], op=ALU.mult)
-            eng.tensor_tensor(out=dk[:, 2], in0=dk[:, 2], in1=nb[:], op=ALU.mult)
             eng.tensor_tensor(out=dk[:, 1], in0=dk[:, 1], in1=al[:], op=ALU.mult)
             dks[pc] = dk
 
-        def weights_v(pc):
-            al = folds[pc][0]
+        def weights_v(pc, which):
+            al, ha, fe, nb = folds[pc]
             dk = dks[pc]
-            nc.vector.scalar_tensor_tensor(out=dk[:, 3], in0=dk[:, 3], scalar=-2.0, in1=al[:], op0=ALU.add, op1=ALU.mult)
-
-        def silu_s2(pc):
-            sn = sil[pc][1]
-            nc.scalar.activation(out=sn[:], in_=sn[:], func=ACT.Identity, scale=1.0, bias=1.0)
-
-        def silu_g3(pc, eng):
-            th, sn = sil[pc]
-            eng.tensor_tensor(out=sn[:], in0=sn[:], in1=th[:], op=ALU.mult)
+            if which == 0:
+                nc.vector.scalar_tensor_tensor(out=dk[:, 0], in0=dk[:, 0], scalar=0.5, in1=nb[:], op0=ALU.add, op1=ALU.mult)
+            elif which == 1:
+                nc.vector.scalar_tensor_tensor(out=dk[:, 2], in0=dk[:, 2], scalar=-0.5, in1=nb[:], op0=ALU.add, op1=ALU.mult)
+            else:
+                nc.vector.scalar_tensor_tensor(out=dk[:, 3], in0=dk[:, 3], scalar=-2.0, in1=al[:], op0=ALU.add, op1=ALU.mult)
 
         def base_pv(pc):
             ib = pc // 2
@@ -195,8 +186,13 @@ def tile_kanlayer_kernel(tc, x, base_w, base_b, spline_w, grad_out, out):
                 start=True,
                 stop=True,
             )
+            tb = work.tile([P, 512], F32, tag="tb", name="tb%d" % pc)
+            nc.vector.scalar_tensor_tensor(out=tb[:], in0=sil[pc][1][:], scalar=1.0, in1=qb[:], op0=ALU.add, op1=ALU.mult)
+            bts[pc] = tb
+
+        def base_g(pc, eng):
             bt = work.tile([P, 512], F32, tag="bt", bufs=3, name="bt%d" % pc)
-            nc.vector.tensor_tensor(out=bt[:], in0=sil[pc][1][:], in1=qb[:], op=ALU.mult)
+            eng.tensor_tensor(out=bt[:], in0=bts[pc][:], in1=sil[pc][0][:], op=ALU.mult)
             bts[pc] = bt
 
         with tc.tile_pool(name="head", bufs=1) as head:
@@ -240,8 +236,8 @@ def tile_kanlayer_kernel(tc, x, base_w, base_b, spline_w, grad_out, out):
             plane_index(0)
             plane_index(1)
             tanh_part(0)
-            fold(0)
             tanh_part(1)
+            fold(0)
             fold(1)
 
             bgrp = work.tile([P, 2048], BF16, tag="grp", bufs=3, name="bgrp", align_bytes=64)
@@ -264,8 +260,6 @@ def tile_kanlayer_kernel(tc, x, base_w, base_b, spline_w, grad_out, out):
             regroup(1, 1)
             silu_g1(1, nc.gpsimd)
             weights_g(1, nc.gpsimd)
-            silu_s2(1)
-            silu_g3(1, nc.gpsimd)
 
         with tc.tile_pool(name="main", bufs=3) as mainp:
             ms = {}
@@ -303,7 +297,7 @@ def tile_kanlayer_kernel(tc, x, base_w, base_b, spline_w, grad_out, out):
                             out=m[:].rearrange("p (r i) -> p r i", r=4),
                             in0=npr[:, :, tq, :],
                             scalar=float(n + 1),
-                            in1=q[:].rearrange("p (i r) -> p r i", r=4),
+                            in1=q[:].rearrange("p (r i) -> p r i", r=4),
                             op0=ALU.is_equal,
                             op1=ALU.mult,
                         )
@@ -377,25 +371,28 @@ def tile_kanlayer_kernel(tc, x, base_w, base_b, spline_w, grad_out, out):
             for j in range(NGRP + 2):
                 pc = j // 4
                 i = j % 4
+                nxt = pc + 1
                 live = j < NGRP
                 if live:
                     mx_and_mask(j, 0)
                 if 0 <= j - 1 < NGRP:
                     class_sums(j - 1, 0)
+                if j == 2:
+                    weights_g(0, nc.vector)
+                    for which in range(3):
+                        weights_v(0, which)
+                    silu_g1(0, nc.vector)
+                    base_pv(0)
+                    base_g(0, nc.vector)
                 if 0 <= j - 2 < NGRP:
                     weigh(j - 2)
                 if live:
                     mx_and_mask(j, 1)
                 if 0 <= j - 1 < NGRP:
                     class_sums(j - 1, 1)
-                if j == 1:
-                    weights_g(0, nc.vector)
-                    silu_g1(0, nc.vector)
-                    nc.vector.scalar_tensor_tensor(
-                        out=sil[0][1][:], in0=sil[0][1][:], scalar=1.0, in1=sil[0][0][:], op0=ALU.add, op1=ALU.mult
-                    )
-                if live and i == 1:
-                    weights_v(pc)
+                qk = (j + 1) // 4
+                if 1 <= qk < NPC and j - (4 * qk - 1) < 3:
+                    weights_v(qk, j - (4 * qk - 1))
                 if live and pc % 2 == 1 and pc // 2 + 1 < NIB:
                     quantise_w(pc // 2 + 1, i)
                 if 0 <= j - 2 < NGRP:
@@ -403,10 +400,9 @@ def tile_kanlayer_kernel(tc, x, base_w, base_b, spline_w, grad_out, out):
                     if (j - 2) % 4 == 3:
                         store((j - 2) // 4)
                 if live and i == 1:
-                    base_pv(pc)
                     if pc + 2 < NPC:
-                        tanh_part(pc + 2)
                         fold(pc + 2)
+                        tanh_part(pc + 2)
                     if pc % 2 == 1 and (pc + 3) // 2 < NIB:
                         regroup((pc + 3) // 2, 0)
                         regroup((pc + 3) // 2, 1)
@@ -415,13 +411,15 @@ def tile_kanlayer_kernel(tc, x, base_w, base_b, spline_w, grad_out, out):
                         regroup((pc + 2) // 2, 3)
                         if (pc + 2) // 2 + 2 < NIB:
                             load_w((pc + 2) // 2 + 2)
+                if live and i == 2 and nxt < NPC:
+                    base_pv(nxt)
+                    base_g(nxt, nc.gpsimd)
                 if live and i == 2 and pc + 2 < NPC:
-                    silu_g1(pc + 2, nc.gpsimd)
                     plane_index(pc + 2)
                     weights_g(pc + 2, nc.gpsimd)
-                    silu_s2(pc + 2)
-                    silu_g3(pc + 2, nc.gpsimd)
-                if j == 3 or j == 11:
-                    ibx = 2 if j == 3 else 3
-                    tpx = xct(ibx)
-                    nc.vector.tensor_copy(out=xc_t[:, ibx, :], in_=tpx[:])
+                    silu_g1(pc + 2, nc.gpsimd)
+                if live and i == 3:
+                    if j == 3 or j == 11:
+                        ibx = 2 if j == 3 else 3
+                        tpx = xct(ibx)
+                        nc.vector.tensor_copy(out=xc_t[:, ibx, :], in_=tpx[:])

from contextlib import ExitStack

import concourse.masks as masks
import concourse.mybir as mybir

F32 = mybir.dt.float32
BF16 = mybir.dt.bfloat16
I32 = mybir.dt.int32
U32 = mybir.dt.uint32
U8 = mybir.dt.uint8
E4 = mybir.dt.float8_e4m3fn_x4
E5 = mybir.dt.float8_e5m2_x4
ALU = mybir.AluOpType
ACT = mybir.ActivationFunctionType

P = 128
BATCH = 1024
IN_F = 512
OUT_F = 512
NG = 13
NT = BATCH // P
NIB = IN_F // P
NPC = 8
NGRP = 32
WCOLS = P * NG
H = 0.4
CN = 6.0 * H * H / ((H + 1e-8) * (2.0 * H + 1e-8) * (3.0 * H + 1e-8))
FLOPS = 2 * BATCH * OUT_F * IN_F * (NG + 1)
PIN = True
RG_ON_VECTOR = ((0, 0), (0, 1), (0, 2), (0, 3))


def tile_kanlayer_kernel(tc, x, base_w, base_b, spline_w, grad_out, out):
    nc = tc.nc
    with ExitStack() as ctx:
        if PIN:
            ctx.enter_context(tc.manual_schedule())
        keep = ctx.enter_context(tc.tile_pool(name="keep", bufs=1))
        work = ctx.enter_context(tc.tile_pool(name="work", bufs=2))
        pq = ctx.enter_context(tc.psum_pool(name="pq", bufs=5))
        psel = ctx.enter_context(tc.psum_pool(name="psel", bufs=2))
        po = ctx.enter_context(tc.psum_pool(name="po", bufs=1))

        ident_b = keep.tile([P, P], BF16, name="ident_b")
        masks.make_identity(nc, ident_b[:])
        ident_f = keep.tile([P, P], F32, name="ident_f")
        masks.make_identity(nc, ident_f[:])

        xc_sb = keep.tile([P, NT, IN_F], BF16, name="xc_sb")
        xc_t = keep.tile([P, NIB, BATCH], BF16, name="xc_t")
        go_codes = keep.tile([P, BATCH], U32, name="go_codes", align_bytes=64)
        go_scales = keep.tile([P, BATCH], U8, name="go_scales", align_bytes=64)
        w_codes = keep.tile([P, NIB, WCOLS], U32, name="w_codes", align_bytes=64)
        w_scales = keep.tile([P, NIB, WCOLS], U8, name="w_scales", align_bytes=64)
        b_codes = keep.tile([P, IN_F], U32, name="b_codes", align_bytes=64)
        b_scales = keep.tile([P, IN_F], U8, name="b_scales", align_bytes=64)

        raws = {}
        grps = {}
        folds = {}
        nprs = {}
        dks = {}
        sil = {}
        bts = {}
        out_v = out.rearrange("(t p) i -> p t i", p=P)

        def load_w(ib):
            raw = work.tile([P, 4, WCOLS], BF16, tag="raw", bufs=2, name="raw%d" % ib)
            for u in range(2):
                nc.sync.dma_start(
                    out=raw[:, 2 * u : 2 * u + 2, :],
                    in_=spline_w[256 * u : 256 * u + 256, ib * P : (ib + 1) * P, :].rearrange("(q e) i g -> q e (i g)", e=2),
                )
            raws[ib] = raw

        def regroup(ib, n):
            rv = raws[ib][:].rearrange("p t (i g) -> p i t g", g=NG)
            if n < 3:
                grp = work.tile([P, 2048], BF16, tag="grp", bufs=3, name="grp%d_%d" % (ib, n), align_bytes=64)
                dst = grp[:].rearrange("p (r i t) -> p i t r", r=4, i=P, t=4)
                src = rv[:, :, :, 4 * n : 4 * n + 4]
            else:
                grp = work.tile([P, 512], BF16, tag="grp12", bufs=2, name="grp12_%d" % ib, align_bytes=64)
                dst = grp[:].rearrange("p (i t o) -> p i t o", t=4, o=1)
                src = rv[:, :, :, 12:13]
            if (ib, n) in RG_ON_VECTOR:
                nc.vector.tensor_copy(out=dst, in_=src)
            else:
                nc.scalar.copy(out=dst, in_=src)
            grps[(ib, n)] = grp

        def quantise_w(ib, n):
            lo = n * 512
            hi = lo + (512 if n < 3 else P)
            nc.vector.quantize_mx(out=w_codes[:, ib, lo:hi].bitcast(E4), scales=w_scales[:, ib, lo:hi], in_=grps[(ib, n)][:])

        def xct(ib):
            tp = pq.tile([P, BATCH], BF16, tag="q", name="tpx%d" % ib)
            for t in range(NT):
                nc.tensor.transpose(out=tp[:, t * P : (t + 1) * P], in_=xc_sb[:, t, ib * P : (ib + 1) * P], identity=ident_b[:])
            return tp

        def fold(pc):
            ib = pc // 2
            hb = pc % 2
            src = xc_t[:, ib, hb * 512 : (hb + 1) * 512]
            fa = work.tile([P, 512], F32, tag="fa", name="fa%d" % pc)
            nc.scalar.activation(out=fa[:], in_=src, func=ACT.Abs, scale=2.5)
            nc.scalar.activation(out=fa[:], in_=fa[:], func=ACT.Abs, bias=-4.0)
            nc.scalar.activation(out=fa[:], in_=fa[:], func=ACT.Abs, bias=-2.0)
            al = work.tile([P, 512], F32, tag="al", name="al%d" % pc)
            nc.scalar.activation(out=al[:], in_=fa[:], func=ACT.Identity, scale=-1.0, bias=1.0)
            ha = work.tile([P, 512], F32, tag="ha", name="ha%d" % pc)
            nc.scalar.activation(out=ha[:], in_=fa[:], func=ACT.Abs, scale=0.5, bias=-0.5)
            fe = work.tile([P, 512], F32, tag="fe", name="fe%d" % pc)
            nc.scalar.activation(out=fe[:], in_=src, func=ACT.Abs, scale=2.5, bias=-1.0)
            nc.scalar.activation(out=fe[:], in_=fe[:], func=ACT.Abs, bias=-4.0)
            nc.scalar.activation(out=fe[:], in_=fe[:], func=ACT.Abs, bias=-2.0)
            nc.scalar.activation(out=fe[:], in_=fe[:], func=ACT.Abs, bias=-2.0)
            nb = work.tile([P, 512], F32, tag="nb", name="nb%d" % pc)
            nc.scalar.activation(out=nb[:], in_=fe[:], func=ACT.Identity, scale=-1.0, bias=1.0)
            folds[pc] = (al, ha, fe, nb)

        def tanh_part(pc):
            ib = pc // 2
            hb = pc % 2
            src = xc_t[:, ib, hb * 512 : (hb + 1) * 512]
            th = work.tile([P, 512], F32, tag="th", name="th%d" % pc)
            nc.scalar.activation(out=th[:], in_=src, func=ACT.Tanh, scale=0.5)
            sn = work.tile([P, 512], F32, tag="sn", name="sn%d" % pc)
            nc.scalar.activation(out=sn[:], in_=th[:], func=ACT.Identity, scale=-0.5, bias=0.5)
            nc.scalar.activation(out=th[:], in_=th[:], func=ACT.Identity, scale=0.5, bias=0.5)
            sil[pc] = (th, sn)

        def plane_index(pc):
            ib = pc // 2
            hb = pc % 2
            npr = work.tile([P, 4, 4, P], I32, tag="npr", bufs=3, name="npr%d" % pc)
            for r in range(4):
                nc.gpsimd.tensor_scalar(
                    out=npr[:, r],
                    in0=xc_sb[:, 4 * hb : 4 * hb + 4, ib * P : (ib + 1) * P],
                    scalar1=0.625,
                    scalar2=(8.0 - r) / 4.0 + 0.5,
                    op0=ALU.mult,
                    op1=ALU.add,
                )
            nprs[pc] = npr

        def silu_g1(pc, eng):
            ib = pc // 2
            hb = pc % 2
            sn = sil[pc][1]
            eng.tensor_tensor(out=sn[:], in0=xc_t[:, ib, hb * 512 : (hb + 1) * 512], in1=sn[:], op=ALU.mult)

        def weights_g(pc, eng):
            al, ha, fe, nb = folds[pc]
            dk = work.tile([P, 4, 512], F32, tag="dk", bufs=4, name="dk%d" % pc)
            eng.tensor_tensor(out=dk[:, 0], in0=al[:], in1=ha[:], op=ALU.add)
            eng.tensor_tensor(out=dk[:, 2], in0=al[:], in1=ha[:], op=ALU.subtract)
            eng.tensor_tensor(out=dk[:, 3], in0=fe[:], in1=ha[:], op=ALU.add)
            eng.tensor_tensor(out=dk[:, 1], in0=fe[:], in1=ha[:], op=ALU.subtract)
            eng.tensor_tensor(out=dk[:, 1], in0=dk[:, 1], in1=al[:], op=ALU.mult)
            dks[pc] = dk

        def weights_v(pc, which):
            al, ha, fe, nb = folds[pc]
            dk = dks[pc]
            if which == 0:
                nc.vector.scalar_tensor_tensor(out=dk[:, 0], in0=dk[:, 0], scalar=0.5, in1=nb[:], op0=ALU.add, op1=ALU.mult)
            elif which == 1:
                nc.vector.scalar_tensor_tensor(out=dk[:, 2], in0=dk[:, 2], scalar=-0.5, in1=nb[:], op0=ALU.add, op1=ALU.mult)
            else:
                nc.vector.scalar_tensor_tensor(out=dk[:, 3], in0=dk[:, 3], scalar=-2.0, in1=al[:], op0=ALU.add, op1=ALU.mult)

        def base_pv(pc):
            ib = pc // 2
            hb = pc % 2
            qb = pq.tile([P, 512], F32, tag="q", name="qb%d" % pc)
            nc.tensor.matmul_mx(
                out=qb[:],
                lhsT=b_codes[:, ib * P : (ib + 1) * P].bitcast(E4),
                lhsT_scale=b_scales[:, ib * P : (ib + 1) * P],
                rhs=go_codes[:, hb * 512 : (hb + 1) * 512].bitcast(E5),
                rhs_scale=go_scales[:, hb * 512 : (hb + 1) * 512],
                start=True,
                stop=True,
            )
            tb = work.tile([P, 512], F32, tag="tb", name="tb%d" % pc)
            nc.vector.scalar_tensor_tensor(out=tb[:], in0=sil[pc][1][:], scalar=1.0, in1=qb[:], op0=ALU.add, op1=ALU.mult)
            bts[pc] = tb

        def base_g(pc, eng):
            bt = work.tile([P, 512], F32, tag="bt", bufs=3, name="bt%d" % pc)
            eng.tensor_tensor(out=bt[:], in0=bts[pc][:], in1=sil[pc][0][:], op=ALU.mult)
            bts[pc] = bt

        with tc.tile_pool(name="head", bufs=1) as head:
            x_sb = head.tile([P, NT, IN_F], BF16, name="x_sb")
            nc.sync.dma_start(out=x_sb[:], in_=x.rearrange("(t p) i -> p t i", p=P))
            go_sb = head.tile([P, NT, OUT_F], BF16, name="go_sb")
            nc.sync.dma_start(out=go_sb[:], in_=grad_out.rearrange("(t p) o -> p t o", p=P))
            load_w(0)
            braw = head.tile([P, 4, IN_F], BF16, name="braw")
            for u in range(2):
                nc.sync.dma_start(
                    out=braw[:, 2 * u : 2 * u + 2, :],
                    in_=base_w[256 * u : 256 * u + 256, :].rearrange("(q e) i -> q e i", e=2),
                )
            load_w(1)

            nc.vector.tensor_scalar(out=xc_sb[:], in0=x_sb[:], scalar1=32.0, scalar2=-32.0, op0=ALU.min, op1=ALU.max)
            tp0 = xct(0)
            nc.scalar.copy(out=xc_t[:, 0, :], in_=tp0[:])

            ggo = head.tile([P, BATCH * 4], BF16, name="ggo", align_bytes=64)
            ggo_f = ggo[:].bitcast(F32).rearrange("p (b u) -> p b u", u=2)
            for pr in range(NT // 2):
                gw = pq.tile([P, 2, 2, P], F32, tag="q", name="gw%d" % pr)
                for tl in range(2):
                    words = go_sb[:, 2 * pr + tl, :].bitcast(F32)
                    for u in range(2):
                        nc.tensor.transpose(out=gw[:, tl, u, :], in_=words[:, u * P : (u + 1) * P], identity=ident_f[:])
                nc.vector.tensor_copy(
                    out=ggo_f[:, pr * 256 : (pr + 1) * 256, :].rearrange("p (tl b) u -> p tl b u", tl=2),
                    in_=gw[:].rearrange("p tl u b -> p tl b u"),
                )
            tp1 = xct(1)
            nc.vector.tensor_copy(out=xc_t[:, 1, :], in_=tp1[:])
            for pr in range(NT // 2):
                nc.vector.quantize_mx(
                    out=go_codes[:, pr * 256 : (pr + 1) * 256].bitcast(E5),
                    scales=go_scales[:, pr * 256 : (pr + 1) * 256],
                    in_=ggo[:, pr * 1024 : (pr + 1) * 1024],
                )
            plane_index(0)
            plane_index(1)
            tanh_part(0)
            tanh_part(1)
            fold(0)
            fold(1)

            bgrp = work.tile([P, 2048], BF16, tag="grp", bufs=3, name="bgrp", align_bytes=64)
            nc.vector.tensor_copy(
                out=bgrp[:].rearrange("p (c i t) -> p c t i", i=4, t=4),
                in_=braw[:].rearrange("p t (c i) -> p c t i", i=4),
            )
            regroup(0, 0)
            nc.vector.quantize_mx(out=b_codes[:].bitcast(E4), scales=b_scales[:], in_=bgrp[:])
            regroup(0, 1)
            quantise_w(0, 0)
            regroup(0, 2)
            quantise_w(0, 1)
            regroup(0, 3)
            quantise_w(0, 2)
            quantise_w(0, 3)
            load_w(2)

            regroup(1, 0)
            regroup(1, 1)
            silu_g1(1, nc.gpsimd)
            weights_g(1, nc.gpsimd)

        with tc.tile_pool(name="main", bufs=3) as mainp:
            ms = {}
            sels = {}
            us = {}
            os_ = {}

            def mx_and_mask(k, half):
                pc = k // 4
                tq = k % 4
                ib = pc // 2
                t = 4 * (pc % 2) + tq
                npr = nprs[pc]
                if half == 0:
                    ms[k] = []
                qs = []
                for n in (2 * half, 2 * half + 1):
                    lo = n * 512 if n < 3 else WCOLS - 512
                    q = pq.tile([P, 512], F32, tag="q", name="q%d_%d" % (k, n))
                    nc.tensor.matmul_mx(
                        out=q[:],
                        lhsT=go_codes[:, t * P : (t + 1) * P].bitcast(E5),
                        lhsT_scale=go_scales[:, t * P : (t + 1) * P],
                        rhs=w_codes[:, ib, lo : lo + 512].bitcast(E4),
                        rhs_scale=w_scales[:, ib, lo : lo + 512],
                        start=True,
                        stop=True,
                    )
                    qs.append(q)
                for n in (2 * half, 2 * half + 1):
                    q = qs[n - 2 * half]
                    if n < 3:
                        m = mainp.tile([P, 512], F32, tag="m", bufs=9, name="m%d_%d" % (k, n))
                        nc.vector.scalar_tensor_tensor(
                            out=m[:].rearrange("p (r i) -> p r i", r=4),
                            in0=npr[:, :, tq, :],
                            scalar=float(n + 1),
                            in1=q[:].rearrange("p (r i) -> p r i", r=4),
                            op0=ALU.is_equal,
                            op1=ALU.mult,
                        )
                    else:
                        m = mainp.tile([P, P], F32, tag="m12", bufs=3, name="m12_%d" % k)
                        nc.vector.scalar_tensor_tensor(
                            out=m[:], in0=npr[:, 0, tq, :], scalar=4.0, in1=q[:, 384:512], op0=ALU.is_equal, op1=ALU.mult
                        )
                    ms[k].append(m)

            def class_sums(k, half):
                if half == 0:
                    sels[k] = psel.tile([P, 512], F32, tag="sel", name="sel%d" % k)
                sel = sels[k]
                for r in (2 * half, 2 * half + 1):
                    terms = [ms[k][n][:, r * P : (r + 1) * P] for n in range(3)]
                    if r == 0:
                        terms.append(ms[k][3][:])
                    for j, term in enumerate(terms):
                        nc.tensor.matmul(
                            out=sel[:, r * P : (r + 1) * P],
                            lhsT=term,
                            rhs=ident_f[:],
                            is_transpose=True,
                            start=(j == 0),
                            stop=(j == len(terms) - 1),
                        )

            def weigh(k):
                pc = k // 4
                tq = k % 4
                uu = mainp.tile([P, 512], F32, tag="u", bufs=3, name="u%d" % k)
                nc.vector.scalar_tensor_tensor(
                    out=uu[:].rearrange("p (r b) -> p r b", r=4),
                    in0=dks[pc][:, :, tq * P : (tq + 1) * P],
                    scalar=CN,
                    in1=sels[k][:].rearrange("p (r b) -> p r b", r=4),
                    op0=ALU.mult,
                    op1=ALU.mult,
                )
                us[k] = uu

            def final_sums(k):
                pc = k // 4
                tq = k % 4
                if tq == 0:
                    os_[pc] = po.tile([P, 512], F32, tag="o", name="o%d" % pc)
                o = os_[pc]
                terms = [us[k][:, r * P : (r + 1) * P] for r in range(4)]
                terms.append(bts[pc][:, tq * P : (tq + 1) * P])
                for j, term in enumerate(terms):
                    nc.tensor.matmul(
                        out=o[:, tq * P : (tq + 1) * P],
                        lhsT=term,
                        rhs=ident_f[:],
                        is_transpose=True,
                        start=(j == 0),
                        stop=(j == len(terms) - 1),
                    )

            def store(pc):
                ib = pc // 2
                hb = pc % 2
                osb = mainp.tile([P, 512], F32, tag="osb", bufs=2, name="osb%d" % pc)
                nc.scalar.copy(out=osb[:], in_=os_[pc][:])
                nc.sync.dma_start(
                    out=out_v[:, 4 * hb : 4 * hb + 4, ib * P : (ib + 1) * P],
                    in_=osb[:].rearrange("p (t i) -> p t i", t=4),
                )

            for j in range(NGRP + 2):
                pc = j // 4
                i = j % 4
                nxt = pc + 1
                live = j < NGRP
                if live:
                    mx_and_mask(j, 0)
                if 0 <= j - 1 < NGRP:
                    class_sums(j - 1, 0)
                if j == 2:
                    weights_g(0, nc.vector)
                    for which in range(3):
                        weights_v(0, which)
                    silu_g1(0, nc.vector)
                    base_pv(0)
                    base_g(0, nc.vector)
                if 0 <= j - 2 < NGRP:
                    weigh(j - 2)
                if live:
                    mx_and_mask(j, 1)
                if 0 <= j - 1 < NGRP:
                    class_sums(j - 1, 1)
                qk = (j + 1) // 4
                if 1 <= qk < NPC and j - (4 * qk - 1) < 3:
                    weights_v(qk, j - (4 * qk - 1))
                if live and pc % 2 == 1 and pc // 2 + 1 < NIB:
                    quantise_w(pc // 2 + 1, i)
                if 0 <= j - 2 < NGRP:
                    final_sums(j - 2)
                    if (j - 2) % 4 == 3:
                        store((j - 2) // 4)
                if live and i == 1:
                    if pc + 2 < NPC:
                        fold(pc + 2)
                        tanh_part(pc + 2)
                    if pc % 2 == 1 and (pc + 3) // 2 < NIB:
                        regroup((pc + 3) // 2, 0)
                        regroup((pc + 3) // 2, 1)
                    if pc % 2 == 0 and (pc + 2) // 2 < NIB:
                        regroup((pc + 2) // 2, 2)
                        regroup((pc + 2) // 2, 3)
                        if (pc + 2) // 2 + 2 < NIB:
                            load_w((pc + 2) // 2 + 2)
                if live and i == 2 and nxt < NPC:
                    base_pv(nxt)
                    base_g(nxt, nc.gpsimd)
                if live and i == 2 and pc + 2 < NPC:
                    plane_index(pc + 2)
                    weights_g(pc + 2, nc.gpsimd)
                    silu_g1(pc + 2, nc.gpsimd)
                if live and i == 3:
                    if j == 3 or j == 11:
                        ibx = 2 if j == 3 else 3
                        tpx = xct(ibx)
                        nc.vector.tensor_copy(out=xc_t[:, ibx, :], in_=tpx[:])
